import numpy as np
import ml_dtypes


def mxq(x, axis, fmt="e4m3"):
    dtype, down = {"e4m3": (ml_dtypes.float8_e4m3fn, 7), "e5m2": (ml_dtypes.float8_e5m2, 14)}[fmt]
    v = np.moveaxis(np.asarray(x, np.float32).astype(ml_dtypes.bfloat16).astype(np.float64), axis, -1)
    blocks = v.reshape(v.shape[:-1] + (-1, 32))
    amax = np.abs(blocks).max(-1, keepdims=True)
    byte = np.maximum(np.where(amax > 0, np.frexp(amax)[1] - 1 + 127, 0) - down, 1)
    scale = np.exp2(byte - 127.0)
    codes = (blocks / scale).astype(np.float32).astype(dtype).astype(np.float64)
    return np.moveaxis((codes * scale).reshape(v.shape), -1, axis)


WIDE = False


def mx_kscale(k):
    if not WIDE:
        return np.ones(k)
    levels = np.array([10, -10, 5, -5, 0])
    a = np.random.permutation(np.resize(levels, k // 512 * 4)).reshape(k // 512, 4)
    idx = np.arange(k)
    return np.exp2(a[idx // 512, idx % 128 // 32])


BF16 = ml_dtypes.bfloat16


def bf(x):
    return np.asarray(x, np.float32).astype(BF16)


def f64(x):
    return np.asarray(x).astype(np.float64)


B, C, T, H = 4, 1536, 512, 512
EPS_LN = 1e-5
EPS_STD = 1e-5


def ln_dim1(z, g, b):
    mu = z.mean(axis=1, keepdims=True)
    var = ((z - mu) ** 2).mean(axis=1, keepdims=True)
    return (z - mu) / np.sqrt(var + EPS_LN) * g[None, :, None] + b[None, :, None]


def stats(x, m):
    mean = (m * x).sum(axis=2)
    std = np.sqrt(np.maximum((m * x * x).sum(axis=2) - mean ** 2, EPS_STD))
    return mean, std


def setup_inputs():
    s = mx_kscale(C)
    lens = np.random.randint(T // 2, T, size=B)
    mask = (np.arange(T)[None, None, :] < lens[:, None, None]) * 1.0
    off = 0.5 * np.random.standard_normal((B, C, 1))
    gain = 0.5 + np.random.random((B, C, 1))
    pad = np.random.standard_normal((B, C, 1)) * (1.0 - mask)
    x = off + gain * np.random.standard_normal((B, C, T)) + pad
    return {"x": bf(x * s[None, :, None]),
            "mask": bf(mask),
            "w1": bf(np.random.standard_normal((H, 3 * C)) / np.sqrt(3 * C) / np.tile(s, 3)[None, :]),
            "b1": bf(0.1 * np.random.standard_normal(H)),
            "g1": bf(1.0 + 0.1 * np.random.standard_normal(H)),
            "be1": bf(0.1 * np.random.standard_normal(H))}


def reference(x, mask, w1, b1, g1, be1):
    x, mask = f64(x), f64(mask)
    total = mask.sum(axis=2, keepdims=True)
    mean0, std0 = stats(x, mask / total)
    mean0 = mean0
    std0 = std0
    x_in = np.concatenate([
        x,
        np.broadcast_to(mean0[:, :, None], (B, C, T)),
        np.broadcast_to(std0[:, :, None], (B, C, T)),
    ], axis=1)
    u = (mxq(f64(w1), 1, "e4m3") @ mxq(x_in, 1, "e4m3")) + f64(b1)[None, :, None]
    return np.tanh(ln_dim1(np.maximum(u, 0.0), f64(g1), f64(be1)))

@@ -1,0 +1,284 @@
+from contextlib import ExitStack
+
+import concourse.mybir as mybir
+from concourse.masks import make_identity
+
+F32 = mybir.dt.float32
+BF16 = mybir.dt.bfloat16
+U32 = mybir.dt.uint32
+U8 = mybir.dt.uint8
+FP8X4 = mybir.dt.float8_e4m3fn_x4
+ALU = mybir.AluOpType
+ACT = mybir.ActivationFunctionType
+AX = mybir.AxisListType
+
+B, C, T, H = 4, 1536, 512, 512
+P = 128
+EPS_LN = 1e-5
+EPS_STD = 1e-5
+FLOPS = 2 * B * H * 3 * C * T
+
+
+def tile_attentivestatspool_pa_kernel(tc, x, mask, w1, b1, g1, be1, out):
+    nc = tc.nc
+    with ExitStack() as ctx:
+        const = ctx.enter_context(tc.tile_pool(name="const", bufs=1))
+        big = ctx.enter_context(tc.tile_pool(name="big", bufs=5))
+        work = ctx.enter_context(tc.tile_pool(name="work", bufs=3))
+        two = ctx.enter_context(tc.tile_pool(name="two", bufs=2))
+        outp = ctx.enter_context(tc.tile_pool(name="outp", bufs=4))
+        ps_a = ctx.enter_context(tc.psum_pool(name="ps_a", bufs=4))
+        ps_b = ctx.enter_context(tc.psum_pool(name="ps_b", bufs=2))
+        ps_c = ctx.enter_context(tc.psum_pool(name="ps_c", bufs=2))
+
+        maskb = const.tile([P, B, T], BF16)
+        nc.sync.dma_start(
+            out=maskb[:].rearrange("p b t -> p (b t)"),
+            in_=mask.rearrange("b o t -> (b o t)").partition_broadcast(P),
+        )
+        prm = const.tile([P, P], BF16)
+        nc.vector.memset(prm[:], 0.0)
+        nc.sync.dma_start(out=prm[0:4, :], in_=b1.rearrange("(r c) -> r c", c=P))
+        nc.sync.dma_start(out=prm[4:8, :], in_=g1.rearrange("(r c) -> r c", c=P))
+        nc.sync.dma_start(out=prm[8:12, :], in_=be1.rearrange("(r c) -> r c", c=P))
+
+        def load_x(b):
+            xt = big.tile([P, 12, T], BF16, tag="big", name="xt%d" % b)
+            for g in range(3):
+                nc.sync.dma_start(
+                    out=xt[:, 4 * g : 4 * g + 4, :].rearrange("p (u e) t -> p u (e t)", u=2),
+                    in_=x[b, 512 * g : 512 * (g + 1), :].rearrange(
+                        "(u p e) t -> p u (e t)", u=2, p=P, e=2
+                    ),
+                )
+            return xt
+
+        def load_w(kc):
+            wt = big.tile([P, 4, C], BF16, tag="big", name="wt%d" % kc)
+            nc.sync.dma_start(
+                out=wt[:],
+                in_=w1[:, C * kc : C * (kc + 1)].rearrange("(a p) k -> p a k", p=P),
+            )
+            return wt
+
+        xts = [load_x(0)]
+        wts = [load_w(kc) for kc in range(3)]
+        xts.append(load_x(1))
+
+        ident_f = const.tile([P, P], F32)
+        make_identity(nc, ident_f[:])
+        ident_b = const.tile([P, P], BF16)
+        make_identity(nc, ident_b[:])
+        sin = const.tile([P, 8, 64, 4], BF16, align_bytes=64)
+        nc.vector.memset(sin[:], 0.0)
+        half = const.tile([P, 12], F32)
+        nc.vector.memset(half[:], 0.5)
+        mhalf = const.tile([P, 4], F32)
+        nc.vector.memset(mhalf[:], -0.5)
+
+        wq = const.tile([P, 9, H], U32, align_bytes=64)
+        wsc = const.tile([P, 9, H], U8, align_bytes=64)
+
+        tot = const.tile([P, B], F32)
+        nc.vector.tensor_reduce(out=tot[:], in_=maskb[:], axis=AX.X, op=ALU.add)
+        rtot = const.tile([P, B], F32)
+        nc.vector.reciprocal(out=rtot[:], in_=tot[:])
+        c256 = const.tile([P, B], F32)
+        nc.vector.tensor_scalar_mul(out=c256[:], in0=rtot[:], scalar1=256.0)
+
+        prm_ps = ps_b.tile([P, P], BF16, tag="mm")
+        nc.tensor.transpose(prm_ps[:], prm[:], ident_b[:])
+        prm_t = const.tile([P, 12], F32)
+        nc.vector.tensor_copy(out=prm_t[:], in_=prm_ps[:, 0:12])
+
+        def stats(b):
+            xt = xts[b]
+            st = two.tile([P, 12, 6], F32, tag="st")
+            for g in range(3):
+                xm = work.tile([P, 4, T], BF16, tag="xm")
+                nc.vector.tensor_tensor(
+                    out=xm[:],
+                    in0=xt[:, 4 * g : 4 * g + 4, :],
+                    in1=maskb[:, b, :].unsqueeze(1).to_broadcast([P, 4, T]),
+                    op=ALU.mult,
+                )
+                for j in range(4):
+                    nc.vector.bn_stats(out=st[:, 4 * g + j, :], in_=xm[:, j, :])
+            return st
+
+        def wprep(g):
+            kc, gl = divmod(g, 3)
+            w32 = wts[kc][:].bitcast(F32)
+            wg = work.tile([P, H, 4], BF16, tag="wg", align_bytes=64)
+            wg32 = wg[:].bitcast(F32)
+            for a2 in range(2):
+                wps = ps_a.tile([P, 2, 256], F32, tag="t1")
+                for u in range(2):
+                    for a in range(2):
+                        c0 = 256 * gl + 128 * u
+                        nc.tensor.transpose(
+                            wps[:, u, 128 * a : 128 * a + 128],
+                            w32[:, 2 * a2 + a, c0 : c0 + 128],
+                            ident_f[:],
+                        )
+                nc.scalar.copy(
+                    out=wg32[:, 256 * a2 : 256 * a2 + 256, :],
+                    in_=wps[:].rearrange("p u n -> p n u"),
+                )
+            nc.vector.quantize_mx(
+                out=wq[:, g, :].bitcast(FP8X4),
+                scales=wsc[:, g, :],
+                in_=wg[:].rearrange("p h j -> p (h j)"),
+            )
+
+        def xprep(b):
+            xt = xts[b]
+            xq = work.tile([P, 3, T], U32, tag="xq", align_bytes=64)
+            xsc = work.tile([P, 3, T], U8, tag="xsc", align_bytes=64)
+            for g in range(3):
+                xg = work.tile([P, T, 4], BF16, tag="xg", align_bytes=64)
+                nc.scalar.copy(
+                    out=xg[:].rearrange("p (c i) j -> p c j i", i=4),
+                    in_=xt[:, 4 * g : 4 * g + 4, :].rearrange("p j (c i) -> p c j i", i=4),
+                )
+                nc.vector.quantize_mx(
+                    out=xq[:, g, :].bitcast(FP8X4),
+                    scales=xsc[:, g, :],
+                    in_=xg[:].rearrange("p t j -> p (t j)"),
+                )
+            return xq, xsc
+
+        def statq(b, st):
+            stv = st[:].rearrange("p r (h s) -> p (r h) s", s=3)
+            mcol = stv[:, :, 1]
+            vcol = stv[:, :, 2]
+            sq = two.tile([P, 24], F32, tag="sq")
+            nc.vector.tensor_tensor(out=sq[:], in0=mcol, in1=mcol, op=ALU.mult)
+            t2 = two.tile([P, 24], F32, tag="t2")
+            nc.vector.scalar_tensor_tensor(
+                out=t2[:], in0=sq[:], scalar=256.0, in1=vcol, op0=ALU.mult, op1=ALU.add
+            )
+            s2 = two.tile([P, 12], F32, tag="s2")
+            nc.vector.tensor_reduce(
+                out=s2[:], in_=t2[:].rearrange("p (r h) -> p r h", h=2), axis=AX.X, op=ALU.add
+            )
+            s1 = two.tile([P, 12], F32, tag="s1")
+            nc.vector.tensor_reduce(
+                out=s1[:], in_=mcol.rearrange("p (r h) -> p r h", h=2), axis=AX.X, op=ALU.add
+            )
+            mean0 = two.tile([P, 12], F32, tag="mean0")
+            nc.vector.tensor_scalar_mul(out=mean0[:], in0=s1[:], scalar1=c256[:, b : b + 1])
+            msq = two.tile([P, 12], F32, tag="msq")
+            nc.vector.tensor_tensor(out=msq[:], in0=mean0[:], in1=mean0[:], op=ALU.mult)
+            var = two.tile([P, 12], F32, tag="var")
+            nc.vector.scalar_tensor_tensor(
+                out=var[:], in0=s2[:], scalar=rtot[:, b : b + 1], in1=msq[:],
+                op0=ALU.mult, op1=ALU.subtract,
+            )
+            varc = two.tile([P, 12], F32, tag="varc")
+            nc.vector.tensor_scalar_max(out=varc[:], in0=var[:], scalar1=EPS_STD)
+            nc.vector.tensor_copy(
+                out=sin[:, 0:3, b, :], in_=mean0[:].rearrange("p (g j) -> p g j", j=4)
+            )
+            nc.gpsimd.tensor_tensor(
+                out=sin[:, 3:6, b, :],
+                in0=varc[:].rearrange("p (g j) -> p g j", j=4),
+                in1=half[:].rearrange("p (g j) -> p g j", j=4),
+                op=ALU.pow,
+            )
+            sqt = two.tile([P, 512], U32, tag="sqt", align_bytes=64)
+            ssc = two.tile([P, 512], U8, tag="ssc", align_bytes=64)
+            nc.vector.quantize_mx(
+                out=sqt[:].bitcast(FP8X4),
+                scales=ssc[:],
+                in_=sin[:].rearrange("p s n j -> p (s n j)"),
+            )
+            ps_s = ps_b.tile([P, 4, P], F32, tag="mm")
+            for ht in range(4):
+                for s in range(6):
+                    nc.tensor.matmul_mx(
+                        out=ps_s[:, ht, :],
+                        lhsT=wq[:, 3 + s, P * ht : P * ht + P].bitcast(FP8X4),
+                        lhsT_scale=wsc[:, 3 + s, P * ht : P * ht + P],
+                        rhs=sqt[:, 64 * s : 64 * s + P].bitcast(FP8X4),
+                        rhs_scale=ssc[:, 64 * s : 64 * s + P],
+                        start=(s == 0),
+                        stop=(s == 5),
+                    )
+            bias = two.tile([P, 4], F32, tag="bias")
+            nc.vector.tensor_tensor(out=bias[:], in0=ps_s[:, :, b], in1=prm_t[:, 0:4], op=ALU.add)
+            return bias
+
+        def main(b, xq, xsc, bias):
+            u = two.tile([P, 4, T], F32, tag="u")
+            for ht in range(4):
+                ps_m = ps_b.tile([P, T], F32, tag="mm")
+                for g in range(3):
+                    nc.tensor.matmul_mx(
+                        out=ps_m[:],
+                        lhsT=wq[:, g, P * ht : P * ht + P].bitcast(FP8X4),
+                        lhsT_scale=wsc[:, g, P * ht : P * ht + P],
+                        rhs=xq[:, g, :].bitcast(FP8X4),
+                        rhs_scale=xsc[:, g, :],
+                        start=(g == 0),
+                        stop=(g == 2),
+                    )
+                nc.scalar.activation(
+                    out=u[:, ht, :], in_=ps_m[:], func=ACT.Relu, bias=bias[:, ht : ht + 1], scale=1.0
+                )
+            return u
+
+        def layer_norm(b, u):
+            lst = two.tile([P, 4, 6], F32, tag="lst")
+            mv = two.tile([P, 4, 2], F32, tag="mv")
+            banks = []
+            for tb in range(4):
+                ps1 = ps_a.tile([P, H], F32, tag="t1")
+                for ht in range(4):
+                    nc.tensor.transpose(
+                        ps1[:, P * ht : P * ht + P], u[:, ht, P * tb : P * tb + P], ident_f[:]
+                    )
+                nc.vector.bn_stats(out=lst[:, tb, :], in_=ps1[:])
+                nc.vector.bn_aggr(out=mv[:, tb, :], in_=lst[:, tb, :])
+                banks.append(ps1)
+            ve = two.tile([P, 4], F32, tag="ve")
+            nc.vector.tensor_scalar_add(out=ve[:], in0=mv[:, :, 1], scalar1=EPS_LN)
+            nm = two.tile([P, 4], F32, tag="nm")
+            nc.vector.tensor_scalar_mul(out=nm[:], in0=mv[:, :, 0], scalar1=-1.0)
+            rstd = two.tile([P, 4], F32, tag="rstd")
+            nc.gpsimd.tensor_tensor(out=rstd[:], in0=ve[:], in1=mhalf[:], op=ALU.pow)
+            nb = two.tile([P, 4], F32, tag="nb")
+            nc.gpsimd.tensor_tensor(out=nb[:], in0=nm[:], in1=rstd[:], op=ALU.mult)
+            zn = two.tile([P, 4, H], F32, tag="zn")
+            for tb in range(4):
+                nc.scalar.activation(
+                    out=zn[:, tb, :], in_=banks[tb][:], func=ACT.Identity,
+                    scale=rstd[:, tb : tb + 1], bias=nb[:, tb : tb + 1],
+                )
+            for ht in range(4):
+                ps2 = ps_c.tile([P, T], F32, tag="t2")
+                for tb in range(4):
+                    nc.tensor.transpose(
+                        ps2[:, P * tb : P * tb + P], zn[:, tb, P * ht : P * ht + P], ident_f[:]
+                    )
+                o = outp.tile([P, T], F32, tag="o")
+                nc.scalar.activation(
+                    out=o[:], in_=ps2[:], func=ACT.Tanh,
+                    scale=prm_t[:, 4 + ht : 5 + ht], bias=prm_t[:, 8 + ht : 9 + ht],
+                )
+                nc.sync.dma_start(out=out[b, P * ht : P * ht + P, :], in_=o[:])
+
+        st = stats(0)
+        for g in range(9):
+            wprep(g)
+        xq, xsc = xprep(0)
+        bias = statq(0, st)
+        for b in range(B):
+            u = main(b, xq, xsc, bias)
+            if b + 2 < B:
+                xts.append(load_x(b + 2))
+            if b + 1 < B:
+                st = stats(b + 1)
+                xq, xsc = xprep(b + 1)
+                bias = statq(b + 1, st)
+            layer_norm(b, u)

@@ -25,17 +25,20 @@ def tile_attentivestatspool_pa_kernel(tc, x, mask, w1, b1, g1, be1, out):
         const = ctx.enter_context(tc.tile_pool(name="const", bufs=1))
         big = ctx.enter_context(tc.tile_pool(name="big", bufs=5))
         work = ctx.enter_context(tc.tile_pool(name="work", bufs=3))
+        four = ctx.enter_context(tc.tile_pool(name="four", bufs=4))
         two = ctx.enter_context(tc.tile_pool(name="two", bufs=2))
         outp = ctx.enter_context(tc.tile_pool(name="outp", bufs=4))
         ps_a = ctx.enter_context(tc.psum_pool(name="ps_a", bufs=4))
         ps_b = ctx.enter_context(tc.psum_pool(name="ps_b", bufs=2))
         ps_c = ctx.enter_context(tc.psum_pool(name="ps_c", bufs=2))
 
+        mrow = const.tile([P, B * T], BF16)
+        nc.vector.memset(mrow[:], 0.0)
+        nc.sync.dma_start(out=mrow[0:1, :], in_=mask.rearrange("b o t -> o (b t)"))
+        ones = const.tile([P, P], BF16)
+        nc.vector.memset(ones[:], 1.0)
         maskb = const.tile([P, B, T], BF16)
-        nc.sync.dma_start(
-            out=maskb[:].rearrange("p b t -> p (b t)"),
-            in_=mask.rearrange("b o t -> (b o t)").partition_broadcast(P),
-        )
+        tot = const.tile([P, B], F32)
         prm = const.tile([P, P], BF16)
         nc.vector.memset(prm[:], 0.0)
         nc.sync.dma_start(out=prm[0:4, :], in_=b1.rearrange("(r c) -> r c", c=P))
@@ -79,37 +82,48 @@ def tile_attentivestatspool_pa_kernel(tc, x, mask, w1, b1, g1, be1, out):
         wq = const.tile([P, 9, H], U32, align_bytes=64)
         wsc = const.tile([P, 9, H], U8, align_bytes=64)
 
-        tot = const.tile([P, B], F32)
-        nc.vector.tensor_reduce(out=tot[:], in_=maskb[:], axis=AX.X, op=ALU.add)
+        for b in range(B):
+            m_ps = ps_b.tile([P, T], F32, tag="mm")
+            nc.tensor.matmul(
+                out=m_ps[:], lhsT=ones[:], rhs=mrow[:, T * b : T * (b + 1)], start=True, stop=True
+            )
+            nc.scalar.activation(
+                out=maskb[:, b, :], in_=m_ps[:], func=ACT.Copy, accum_out=tot[:, b : b + 1]
+            )
         rtot = const.tile([P, B], F32)
-        nc.vector.reciprocal(out=rtot[:], in_=tot[:])
         c256 = const.tile([P, B], F32)
-        nc.vector.tensor_scalar_mul(out=c256[:], in0=rtot[:], scalar1=256.0)
 
         prm_ps = ps_b.tile([P, P], BF16, tag="mm")
         nc.tensor.transpose(prm_ps[:], prm[:], ident_b[:])
         prm_t = const.tile([P, 12], F32)
-        nc.vector.tensor_copy(out=prm_t[:], in_=prm_ps[:, 0:12])
 
-        def stats(b):
-            xt = xts[b]
-            st = two.tile([P, 12, 6], F32, tag="st")
-            for g in range(3):
-                xm = work.tile([P, 4, T], BF16, tag="xm")
-                nc.vector.tensor_tensor(
-                    out=xm[:],
-                    in0=xt[:, 4 * g : 4 * g + 4, :],
-                    in1=maskb[:, b, :].unsqueeze(1).to_broadcast([P, 4, T]),
-                    op=ALU.mult,
-                )
-                for j in range(4):
-                    nc.vector.bn_stats(out=st[:, 4 * g + j, :], in_=xm[:, j, :])
-            return st
+        sts = {}
+        xgs = {}
+        xqs = {}
+        wgs = {}
+        sqs = {}
+        biases = {}
+        us = {}
 
-        def wprep(g):
+        def s_unit(b, g):
+            if g == 0:
+                st_new = two.tile([P, 12, 6], F32, tag="st")
+                sts[b] = st_new
+            xm = two.tile([P, 4, T], BF16, tag="xm")
+            nc.vector.tensor_tensor(
+                out=xm[:],
+                in0=xts[b][:, 4 * g : 4 * g + 4, :],
+                in1=maskb[:, b, :].unsqueeze(1).to_broadcast([P, 4, T]),
+                op=ALU.mult,
+            )
+            for j in range(4):
+                nc.vector.bn_stats(out=sts[b][:, 4 * g + j, :], in_=xm[:, j, :])
+
+        def wt_unit(g):
             kc, gl = divmod(g, 3)
             w32 = wts[kc][:].bitcast(F32)
-            wg = work.tile([P, H, 4], BF16, tag="wg", align_bytes=64)
+            wg = four.tile([P, H, 4], BF16, tag="wg", align_bytes=64)
+            wgs[g] = wg
             wg32 = wg[:].bitcast(F32)
             for a2 in range(2):
                 wps = ps_a.tile([P, 2, 256], F32, tag="t1")
@@ -125,31 +139,36 @@ def tile_attentivestatspool_pa_kernel(tc, x, mask, w1, b1, g1, be1, out):
                     out=wg32[:, 256 * a2 : 256 * a2 + 256, :],
                     in_=wps[:].rearrange("p u n -> p n u"),
                 )
+
+        def qw(g):
             nc.vector.quantize_mx(
                 out=wq[:, g, :].bitcast(FP8X4),
                 scales=wsc[:, g, :],
-                in_=wg[:].rearrange("p h j -> p (h j)"),
+                in_=wgs[g][:].rearrange("p h j -> p (h j)"),
             )
 
-        def xprep(b):
-            xt = xts[b]
-            xq = work.tile([P, 3, T], U32, tag="xq", align_bytes=64)
-            xsc = work.tile([P, 3, T], U8, tag="xsc", align_bytes=64)
-            for g in range(3):
-                xg = work.tile([P, T, 4], BF16, tag="xg", align_bytes=64)
-                nc.scalar.copy(
-                    out=xg[:].rearrange("p (c i) j -> p c j i", i=4),
-                    in_=xt[:, 4 * g : 4 * g + 4, :].rearrange("p j (c i) -> p c j i", i=4),
-                )
-                nc.vector.quantize_mx(
-                    out=xq[:, g, :].bitcast(FP8X4),
-                    scales=xsc[:, g, :],
-                    in_=xg[:].rearrange("p t j -> p (t j)"),
-                )
-            return xq, xsc
+        def rg(b, g):
+            xg = work.tile([P, T, 4], BF16, tag="xg", align_bytes=64)
+            xgs[(b, g)] = xg
+            nc.scalar.copy(
+                out=xg[:].rearrange("p (c i) j -> p c j i", i=4),
+                in_=xts[b][:, 4 * g : 4 * g + 4, :].rearrange("p j (c i) -> p c j i", i=4),
+            )
 
-        def statq(b, st):
-            stv = st[:].rearrange("p r (h s) -> p (r h) s", s=3)
+        def qx(b, g):
+            if g == 0:
+                xq_new = work.tile([P, 3, T], U32, tag="xq", align_bytes=64)
+                xsc_new = work.tile([P, 3, T], U8, tag="xsc", align_bytes=64)
+                xqs[b] = (xq_new, xsc_new)
+            xq, xsc = xqs[b]
+            nc.vector.quantize_mx(
+                out=xq[:, g, :].bitcast(FP8X4),
+                scales=xsc[:, g, :],
+                in_=xgs[(b, g)][:].rearrange("p t j -> p (t j)"),
+            )
+
+        def a_step(b):
+            stv = sts[b][:].rearrange("p r (h s) -> p (r h) s", s=3)
             mcol = stv[:, :, 1]
             vcol = stv[:, :, 2]
             sq = two.tile([P, 24], F32, tag="sq")
@@ -177,15 +196,17 @@ def tile_attentivestatspool_pa_kernel(tc, x, mask, w1, b1, g1, be1, out):
             )
             varc = two.tile([P, 12], F32, tag="varc")
             nc.vector.tensor_scalar_max(out=varc[:], in0=var[:], scalar1=EPS_STD)
-            nc.vector.tensor_copy(
-                out=sin[:, 0:3, b, :], in_=mean0[:].rearrange("p (g j) -> p g j", j=4)
-            )
             nc.gpsimd.tensor_tensor(
                 out=sin[:, 3:6, b, :],
                 in0=varc[:].rearrange("p (g j) -> p g j", j=4),
                 in1=half[:].rearrange("p (g j) -> p g j", j=4),
                 op=ALU.pow,
             )
+            nc.vector.tensor_copy(
+                out=sin[:, 0:3, b, :], in_=mean0[:].rearrange("p (g j) -> p g j", j=4)
+            )
+
+        def qs(b):
             sqt = two.tile([P, 512], U32, tag="sqt", align_bytes=64)
             ssc = two.tile([P, 512], U8, tag="ssc", align_bytes=64)
             nc.vector.quantize_mx(
@@ -194,6 +215,7 @@ def tile_attentivestatspool_pa_kernel(tc, x, mask, w1, b1, g1, be1, out):
                 in_=sin[:].rearrange("p s n j -> p (s n j)"),
             )
             ps_s = ps_b.tile([P, 4, P], F32, tag="mm")
+            sqs[b] = ps_s
             for ht in range(4):
                 for s in range(6):
                     nc.tensor.matmul_mx(
@@ -205,12 +227,15 @@ def tile_attentivestatspool_pa_kernel(tc, x, mask, w1, b1, g1, be1, out):
                         start=(s == 0),
                         stop=(s == 5),
                     )
-            bias = two.tile([P, 4], F32, tag="bias")
-            nc.vector.tensor_tensor(out=bias[:], in0=ps_s[:, :, b], in1=prm_t[:, 0:4], op=ALU.add)
-            return bias
 
-        def main(b, xq, xsc, bias):
-            u = two.tile([P, 4, T], F32, tag="u")
+        def main(b):
+            bias = two.tile([P, 4], F32, tag="bias")
+            nc.vector.tensor_tensor(
+                out=bias[:], in0=sqs[b][:, :, b], in1=prm_t[:, 0:4], op=ALU.add
+            )
+            xq, xsc = xqs[b]
+            u = work.tile([P, 4, T], F32, tag="u")
+            us[b] = u
             for ht in range(4):
                 ps_m = ps_b.tile([P, T], F32, tag="mm")
                 for g in range(3):
@@ -226,35 +251,37 @@ def tile_attentivestatspool_pa_kernel(tc, x, mask, w1, b1, g1, be1, out):
                 nc.scalar.activation(
                     out=u[:, ht, :], in_=ps_m[:], func=ACT.Relu, bias=bias[:, ht : ht + 1], scale=1.0
                 )
-            return u
 
-        def layer_norm(b, u):
-            lst = two.tile([P, 4, 6], F32, tag="lst")
-            mv = two.tile([P, 4, 2], F32, tag="mv")
-            banks = []
-            for tb in range(4):
-                ps1 = ps_a.tile([P, H], F32, tag="t1")
-                for ht in range(4):
-                    nc.tensor.transpose(
-                        ps1[:, P * ht : P * ht + P], u[:, ht, P * tb : P * tb + P], ident_f[:]
-                    )
-                nc.vector.bn_stats(out=lst[:, tb, :], in_=ps1[:])
-                nc.vector.bn_aggr(out=mv[:, tb, :], in_=lst[:, tb, :])
-                banks.append(ps1)
-            ve = two.tile([P, 4], F32, tag="ve")
-            nc.vector.tensor_scalar_add(out=ve[:], in0=mv[:, :, 1], scalar1=EPS_LN)
-            nm = two.tile([P, 4], F32, tag="nm")
-            nc.vector.tensor_scalar_mul(out=nm[:], in0=mv[:, :, 0], scalar1=-1.0)
-            rstd = two.tile([P, 4], F32, tag="rstd")
-            nc.gpsimd.tensor_tensor(out=rstd[:], in0=ve[:], in1=mhalf[:], op=ALU.pow)
-            nb = two.tile([P, 4], F32, tag="nb")
-            nc.gpsimd.tensor_tensor(out=nb[:], in0=nm[:], in1=rstd[:], op=ALU.mult)
+        def layer_norm(b):
+            u = us[b]
             zn = two.tile([P, 4, H], F32, tag="zn")
-            for tb in range(4):
-                nc.scalar.activation(
-                    out=zn[:, tb, :], in_=banks[tb][:], func=ACT.Identity,
-                    scale=rstd[:, tb : tb + 1], bias=nb[:, tb : tb + 1],
-                )
+            for pair in range(2):
+                lst = four.tile([P, 2, 6], F32, tag="lst")
+                mv = four.tile([P, 2, 2], F32, tag="mv")
+                pbanks = []
+                for i in range(2):
+                    tb = 2 * pair + i
+                    ps1 = ps_a.tile([P, H], F32, tag="t1")
+                    for ht in range(4):
+                        nc.tensor.transpose(
+                            ps1[:, P * ht : P * ht + P], u[:, ht, P * tb : P * tb + P], ident_f[:]
+                        )
+                    nc.vector.bn_stats(out=lst[:, i, :], in_=ps1[:])
+                    nc.vector.bn_aggr(out=mv[:, i, :], in_=lst[:, i, :])
+                    pbanks.append(ps1)
+                ve = four.tile([P, 2], F32, tag="ve")
+                nc.vector.tensor_scalar_add(out=ve[:], in0=mv[:, :, 1], scalar1=EPS_LN)
+                nm = four.tile([P, 2], F32, tag="nm")
+                nc.vector.tensor_scalar_mul(out=nm[:], in0=mv[:, :, 0], scalar1=-1.0)
+                rstd = four.tile([P, 2], F32, tag="rstd")
+                nc.gpsimd.tensor_tensor(out=rstd[:], in0=ve[:], in1=mhalf[:, 0:2], op=ALU.pow)
+                nb = four.tile([P, 2], F32, tag="nb")
+                nc.gpsimd.tensor_tensor(out=nb[:], in0=nm[:], in1=rstd[:], op=ALU.mult)
+                for i in range(2):
+                    nc.scalar.activation(
+                        out=zn[:, 2 * pair + i, :], in_=pbanks[i][:], func=ACT.Identity,
+                        scale=rstd[:, i : i + 1], bias=nb[:, i : i + 1],
+                    )
             for ht in range(4):
                 ps2 = ps_c.tile([P, T], F32, tag="t2")
                 for tb in range(4):
@@ -268,17 +295,36 @@ def tile_attentivestatspool_pa_kernel(tc, x, mask, w1, b1, g1, be1, out):
                 )
                 nc.sync.dma_start(out=out[b, P * ht : P * ht + P, :], in_=o[:])
 
-        st = stats(0)
+        for g in range(3):
+            rg(0, g)
+            s_unit(0, g)
+        xts.append(load_x(2))
+        nc.vector.tensor_copy(out=prm_t[:], in_=prm_ps[:, 0:12])
+        nc.vector.reciprocal(out=rtot[:], in_=tot[:])
+        nc.vector.tensor_scalar_mul(out=c256[:], in0=rtot[:], scalar1=256.0)
+        a_step(0)
         for g in range(9):
-            wprep(g)
-        xq, xsc = xprep(0)
-        bias = statq(0, st)
-        for b in range(B):
-            u = main(b, xq, xsc, bias)
-            if b + 2 < B:
-                xts.append(load_x(b + 2))
-            if b + 1 < B:
-                st = stats(b + 1)
-                xq, xsc = xprep(b + 1)
-                bias = statq(b + 1, st)
-            layer_norm(b, u)
+            wt_unit(g)
+            qw(g)
+            if g == 2:
+                xts.append(load_x(3))
+        for g in range(3):
+            qx(0, g)
+        qs(0)
+        main(0)
+        for b in range(1, B):
+            for g in range(3):
+                rg(b, g)
+                s_unit(b, g)
+                if b == 3 and g == 0:
+                    layer_norm(1)
+            if b == 2:
+                layer_norm(0)
+            a_step(b)
+            for g in range(3):
+                qx(b, g)
+            qs(b)
+            if b == 3:
+                layer_norm(2)
+            main(b)
+        layer_norm(3)

@@ -41,9 +41,9 @@ def tile_attentivestatspool_pa_kernel(tc, x, mask, w1, b1, g1, be1, out):
         tot = const.tile([P, B], F32)
         prm = const.tile([P, P], BF16)
         nc.vector.memset(prm[:], 0.0)
-        nc.sync.dma_start(out=prm[0:4, :], in_=b1.rearrange("(r c) -> r c", c=P))
-        nc.sync.dma_start(out=prm[4:8, :], in_=g1.rearrange("(r c) -> r c", c=P))
-        nc.sync.dma_start(out=prm[8:12, :], in_=be1.rearrange("(r c) -> r c", c=P))
+        nc.gpsimd.dma_start(out=prm[0:4, :], in_=b1.rearrange("(r c) -> r c", c=P))
+        nc.gpsimd.dma_start(out=prm[4:8, :], in_=g1.rearrange("(r c) -> r c", c=P))
+        nc.gpsimd.dma_start(out=prm[8:12, :], in_=be1.rearrange("(r c) -> r c", c=P))
 
         def load_x(b):
             xt = big.tile([P, 12, T], BF16, tag="big", name="xt%d" % b)
@@ -98,6 +98,7 @@ def tile_attentivestatspool_pa_kernel(tc, x, mask, w1, b1, g1, be1, out):
         prm_t = const.tile([P, 12], F32)
 
         sts = {}
+        xms = {}
         xgs = {}
         xqs = {}
         wgs = {}
@@ -105,19 +106,22 @@ def tile_attentivestatspool_pa_kernel(tc, x, mask, w1, b1, g1, be1, out):
         biases = {}
         us = {}
 
-        def s_unit(b, g):
-            if g == 0:
-                st_new = two.tile([P, 12, 6], F32, tag="st")
-                sts[b] = st_new
-            xm = two.tile([P, 4, T], BF16, tag="xm")
+        def mask_unit(b, g):
+            xm = work.tile([P, 4, T], BF16, tag="xm")
+            xms[(b, g)] = xm
             nc.vector.tensor_tensor(
                 out=xm[:],
                 in0=xts[b][:, 4 * g : 4 * g + 4, :],
                 in1=maskb[:, b, :].unsqueeze(1).to_broadcast([P, 4, T]),
                 op=ALU.mult,
             )
+
+        def bn_unit(b, g):
+            if g == 0:
+                st_new = two.tile([P, 12, 6], F32, tag="st")
+                sts[b] = st_new
             for j in range(4):
-                nc.vector.bn_stats(out=sts[b][:, 4 * g + j, :], in_=xm[:, j, :])
+                nc.vector.bn_stats(out=sts[b][:, 4 * g + j, :], in_=xms[(b, g)][:, j, :])
 
         def wt_unit(g):
             kc, gl = divmod(g, 3)
@@ -171,39 +175,48 @@ def tile_attentivestatspool_pa_kernel(tc, x, mask, w1, b1, g1, be1, out):
             stv = sts[b][:].rearrange("p r (h s) -> p (r h) s", s=3)
             mcol = stv[:, :, 1]
             vcol = stv[:, :, 2]
+            m256 = two.tile([P, 24], F32, tag="m256")
+            nc.gpsimd.tensor_scalar(
+                out=m256[:], in0=mcol, scalar1=256.0, scalar2=0.0, op0=ALU.mult, op1=ALU.add
+            )
             sq = two.tile([P, 24], F32, tag="sq")
-            nc.vector.tensor_tensor(out=sq[:], in0=mcol, in1=mcol, op=ALU.mult)
-            t2 = two.tile([P, 24], F32, tag="t2")
-            nc.vector.scalar_tensor_tensor(
-                out=t2[:], in0=sq[:], scalar=256.0, in1=vcol, op0=ALU.mult, op1=ALU.add
+            nc.gpsimd.tensor_tensor(out=sq[:], in0=m256[:], in1=mcol, op=ALU.mult)
+            t3 = two.tile([P, 12, 2], F32, tag="t3")
+            nc.gpsimd.tensor_tensor(
+                out=t3[:].rearrange("p r h -> p (r h)"), in0=sq[:], in1=vcol, op=ALU.add
             )
             s2 = two.tile([P, 12], F32, tag="s2")
-            nc.vector.tensor_reduce(
-                out=s2[:], in_=t2[:].rearrange("p (r h) -> p r h", h=2), axis=AX.X, op=ALU.add
-            )
+            nc.gpsimd.tensor_tensor(out=s2[:], in0=t3[:, :, 0], in1=t3[:, :, 1], op=ALU.add)
+            m2 = mcol.rearrange("p (r h) -> p r h", h=2)
             s1 = two.tile([P, 12], F32, tag="s1")
-            nc.vector.tensor_reduce(
-                out=s1[:], in_=mcol.rearrange("p (r h) -> p r h", h=2), axis=AX.X, op=ALU.add
-            )
+            nc.gpsimd.tensor_tensor(out=s1[:], in0=m2[:, :, 0], in1=m2[:, :, 1], op=ALU.add)
             mean0 = two.tile([P, 12], F32, tag="mean0")
-            nc.vector.tensor_scalar_mul(out=mean0[:], in0=s1[:], scalar1=c256[:, b : b + 1])
-            msq = two.tile([P, 12], F32, tag="msq")
-            nc.vector.tensor_tensor(out=msq[:], in0=mean0[:], in1=mean0[:], op=ALU.mult)
-            var = two.tile([P, 12], F32, tag="var")
-            nc.vector.scalar_tensor_tensor(
-                out=var[:], in0=s2[:], scalar=rtot[:, b : b + 1], in1=msq[:],
-                op0=ALU.mult, op1=ALU.subtract,
+            nc.gpsimd.tensor_scalar(
+                out=mean0[:], in0=s1[:], scalar1=c256[:, b : b + 1], scalar2=0.0,
+                op0=ALU.mult, op1=ALU.add,
             )
+            nc.gpsimd.tensor_scalar(
+                out=sin[:, 0:3, b, :], in0=mean0[:].rearrange("p (g j) -> p g j", j=4),
+                scalar1=1.0, scalar2=0.0, op0=ALU.mult, op1=ALU.add,
+            )
+            e2 = two.tile([P, 12], F32, tag="e2")
+            nc.gpsimd.tensor_scalar(
+                out=e2[:], in0=s2[:], scalar1=rtot[:, b : b + 1], scalar2=0.0,
+                op0=ALU.mult, op1=ALU.add,
+            )
+            msq = two.tile([P, 12], F32, tag="msq")
+            nc.gpsimd.tensor_tensor(out=msq[:], in0=mean0[:], in1=mean0[:], op=ALU.mult)
+            var = two.tile([P, 12], F32, tag="var")
+            nc.gpsimd.tensor_tensor(out=var[:], in0=e2[:], in1=msq[:], op=ALU.subtract)
             varc = two.tile([P, 12], F32, tag="varc")
-            nc.vector.tensor_scalar_max(out=varc[:], in0=var[:], scalar1=EPS_STD)
+            nc.gpsimd.tensor_scalar(
+                out=varc[:], in0=var[:], scalar1=3.0e38, scalar2=EPS_STD, op0=ALU.min, op1=ALU.max
+            )
             nc.gpsimd.tensor_tensor(
                 out=sin[:, 3:6, b, :],
                 in0=varc[:].rearrange("p (g j) -> p g j", j=4),
                 in1=half[:].rearrange("p (g j) -> p g j", j=4),
                 op=ALU.pow,
-            )
-            nc.vector.tensor_copy(
-                out=sin[:, 0:3, b, :], in_=mean0[:].rearrange("p (g j) -> p g j", j=4)
             )
 
         def qs(b):
@@ -267,16 +280,21 @@ def tile_attentivestatspool_pa_kernel(tc, x, mask, w1, b1, g1, be1, out):
                             ps1[:, P * ht : P * ht + P], u[:, ht, P * tb : P * tb + P], ident_f[:]
                         )
                     nc.vector.bn_stats(out=lst[:, i, :], in_=ps1[:])
-                    nc.vector.bn_aggr(out=mv[:, i, :], in_=lst[:, i, :])
                     pbanks.append(ps1)
+                for i in range(2):
+                    nc.vector.bn_aggr(out=mv[:, i, :], in_=lst[:, i, :])
                 ve = four.tile([P, 2], F32, tag="ve")
-                nc.vector.tensor_scalar_add(out=ve[:], in0=mv[:, :, 1], scalar1=EPS_LN)
-                nm = four.tile([P, 2], F32, tag="nm")
-                nc.vector.tensor_scalar_mul(out=nm[:], in0=mv[:, :, 0], scalar1=-1.0)
+                nc.gpsimd.tensor_scalar(
+                    out=ve[:], in0=mv[:, :, 1], scalar1=EPS_LN, scalar2=1.0, op0=ALU.add, op1=ALU.mult
+                )
                 rstd = four.tile([P, 2], F32, tag="rstd")
                 nc.gpsimd.tensor_tensor(out=rstd[:], in0=ve[:], in1=mhalf[:, 0:2], op=ALU.pow)
+                nm = four.tile([P, 2], F32, tag="nm")
+                nc.gpsimd.tensor_tensor(out=nm[:], in0=mv[:, :, 0], in1=rstd[:], op=ALU.mult)
                 nb = four.tile([P, 2], F32, tag="nb")
-                nc.gpsimd.tensor_tensor(out=nb[:], in0=nm[:], in1=rstd[:], op=ALU.mult)
+                nc.gpsimd.tensor_scalar(
+                    out=nb[:], in0=nm[:], scalar1=-1.0, scalar2=0.0, op0=ALU.mult, op1=ALU.add
+                )
                 for i in range(2):
                     nc.scalar.activation(
                         out=zn[:, 2 * pair + i, :], in_=pbanks[i][:], func=ACT.Identity,
@@ -295,13 +313,23 @@ def tile_attentivestatspool_pa_kernel(tc, x, mask, w1, b1, g1, be1, out):
                 )
                 nc.sync.dma_start(out=out[b, P * ht : P * ht + P, :], in_=o[:])
 
+        units = [(b, g) for b in range(B) for g in range(3)]
+
+        def s_unit(k):
+            if k + 1 < len(units):
+                mask_unit(units[k + 1][0], units[k + 1][1])
+            bn_unit(units[k][0], units[k][1])
+
+        mask_unit(0, 0)
         for g in range(3):
             rg(0, g)
-            s_unit(0, g)
-        xts.append(load_x(2))
+        s_unit(0)
+        s_unit(1)
         nc.vector.tensor_copy(out=prm_t[:], in_=prm_ps[:, 0:12])
         nc.vector.reciprocal(out=rtot[:], in_=tot[:])
         nc.vector.tensor_scalar_mul(out=c256[:], in0=rtot[:], scalar1=256.0)
+        s_unit(2)
+        xts.append(load_x(2))
         a_step(0)
         for g in range(9):
             wt_unit(g)
@@ -315,7 +343,7 @@ def tile_attentivestatspool_pa_kernel(tc, x, mask, w1, b1, g1, be1, out):
         for b in range(1, B):
             for g in range(3):
                 rg(b, g)
-                s_unit(b, g)
+                s_unit(3 * b + g)
                 if b == 3 and g == 0:
                     layer_norm(1)
             if b == 2:

@@ -41,9 +41,9 @@ def tile_attentivestatspool_pa_kernel(tc, x, mask, w1, b1, g1, be1, out):
         tot = const.tile([P, B], F32)
         prm = const.tile([P, P], BF16)
         nc.vector.memset(prm[:], 0.0)
-        nc.gpsimd.dma_start(out=prm[0:4, :], in_=b1.rearrange("(r c) -> r c", c=P))
-        nc.gpsimd.dma_start(out=prm[4:8, :], in_=g1.rearrange("(r c) -> r c", c=P))
-        nc.gpsimd.dma_start(out=prm[8:12, :], in_=be1.rearrange("(r c) -> r c", c=P))
+        warm = const.tile([P, 1], F32)
+        nc.vector.memset(warm[:], 0.0)
+        nc.scalar.activation(out=warm[:], in_=warm[:], func=ACT.Tanh)
 
         def load_x(b):
             xt = big.tile([P, 12, T], BF16, tag="big", name="xt%d" % b)
@@ -67,6 +67,9 @@ def tile_attentivestatspool_pa_kernel(tc, x, mask, w1, b1, g1, be1, out):
         xts = [load_x(0)]
         wts = [load_w(kc) for kc in range(3)]
         xts.append(load_x(1))
+        nc.sync.dma_start(out=prm[0:4, :], in_=b1.rearrange("(r c) -> r c", c=P))
+        nc.sync.dma_start(out=prm[4:8, :], in_=g1.rearrange("(r c) -> r c", c=P))
+        nc.sync.dma_start(out=prm[8:12, :], in_=be1.rearrange("(r c) -> r c", c=P))
 
         ident_f = const.tile([P, P], F32)
         make_identity(nc, ident_f[:])
@@ -93,12 +96,9 @@ def tile_attentivestatspool_pa_kernel(tc, x, mask, w1, b1, g1, be1, out):
         rtot = const.tile([P, B], F32)
         c256 = const.tile([P, B], F32)
 
-        prm_ps = ps_b.tile([P, P], BF16, tag="mm")
-        nc.tensor.transpose(prm_ps[:], prm[:], ident_b[:])
         prm_t = const.tile([P, 12], F32)
 
         sts = {}
-        xms = {}
         xgs = {}
         xqs = {}
         wgs = {}
@@ -106,22 +106,19 @@ def tile_attentivestatspool_pa_kernel(tc, x, mask, w1, b1, g1, be1, out):
         biases = {}
         us = {}
 
-        def mask_unit(b, g):
-            xm = work.tile([P, 4, T], BF16, tag="xm")
-            xms[(b, g)] = xm
+        def s_unit(b, g):
+            if g == 0:
+                st_new = two.tile([P, 12, 6], F32, tag="st")
+                sts[b] = st_new
+            xm = two.tile([P, 4, T], BF16, tag="xm")
             nc.vector.tensor_tensor(
                 out=xm[:],
                 in0=xts[b][:, 4 * g : 4 * g + 4, :],
                 in1=maskb[:, b, :].unsqueeze(1).to_broadcast([P, 4, T]),
                 op=ALU.mult,
             )
-
-        def bn_unit(b, g):
-            if g == 0:
-                st_new = two.tile([P, 12, 6], F32, tag="st")
-                sts[b] = st_new
             for j in range(4):
-                nc.vector.bn_stats(out=sts[b][:, 4 * g + j, :], in_=xms[(b, g)][:, j, :])
+                nc.vector.bn_stats(out=sts[b][:, 4 * g + j, :], in_=xm[:, j, :])
 
         def wt_unit(g):
             kc, gl = divmod(g, 3)
@@ -175,48 +172,39 @@ def tile_attentivestatspool_pa_kernel(tc, x, mask, w1, b1, g1, be1, out):
             stv = sts[b][:].rearrange("p r (h s) -> p (r h) s", s=3)
             mcol = stv[:, :, 1]
             vcol = stv[:, :, 2]
-            m256 = two.tile([P, 24], F32, tag="m256")
-            nc.gpsimd.tensor_scalar(
-                out=m256[:], in0=mcol, scalar1=256.0, scalar2=0.0, op0=ALU.mult, op1=ALU.add
-            )
             sq = two.tile([P, 24], F32, tag="sq")
-            nc.gpsimd.tensor_tensor(out=sq[:], in0=m256[:], in1=mcol, op=ALU.mult)
-            t3 = two.tile([P, 12, 2], F32, tag="t3")
-            nc.gpsimd.tensor_tensor(
-                out=t3[:].rearrange("p r h -> p (r h)"), in0=sq[:], in1=vcol, op=ALU.add
+            nc.vector.tensor_tensor(out=sq[:], in0=mcol, in1=mcol, op=ALU.mult)
+            t2 = two.tile([P, 24], F32, tag="t2")
+            nc.vector.scalar_tensor_tensor(
+                out=t2[:], in0=sq[:], scalar=256.0, in1=vcol, op0=ALU.mult, op1=ALU.add
             )
             s2 = two.tile([P, 12], F32, tag="s2")
-            nc.gpsimd.tensor_tensor(out=s2[:], in0=t3[:, :, 0], in1=t3[:, :, 1], op=ALU.add)
-            m2 = mcol.rearrange("p (r h) -> p r h", h=2)
+            nc.vector.tensor_reduce(
+                out=s2[:], in_=t2[:].rearrange("p (r h) -> p r h", h=2), axis=AX.X, op=ALU.add
+            )
             s1 = two.tile([P, 12], F32, tag="s1")
-            nc.gpsimd.tensor_tensor(out=s1[:], in0=m2[:, :, 0], in1=m2[:, :, 1], op=ALU.add)
+            nc.vector.tensor_reduce(
+                out=s1[:], in_=mcol.rearrange("p (r h) -> p r h", h=2), axis=AX.X, op=ALU.add
+            )
             mean0 = two.tile([P, 12], F32, tag="mean0")
-            nc.gpsimd.tensor_scalar(
-                out=mean0[:], in0=s1[:], scalar1=c256[:, b : b + 1], scalar2=0.0,
-                op0=ALU.mult, op1=ALU.add,
-            )
-            nc.gpsimd.tensor_scalar(
-                out=sin[:, 0:3, b, :], in0=mean0[:].rearrange("p (g j) -> p g j", j=4),
-                scalar1=1.0, scalar2=0.0, op0=ALU.mult, op1=ALU.add,
-            )
-            e2 = two.tile([P, 12], F32, tag="e2")
-            nc.gpsimd.tensor_scalar(
-                out=e2[:], in0=s2[:], scalar1=rtot[:, b : b + 1], scalar2=0.0,
-                op0=ALU.mult, op1=ALU.add,
-            )
+            nc.vector.tensor_scalar_mul(out=mean0[:], in0=s1[:], scalar1=c256[:, b : b + 1])
             msq = two.tile([P, 12], F32, tag="msq")
-            nc.gpsimd.tensor_tensor(out=msq[:], in0=mean0[:], in1=mean0[:], op=ALU.mult)
+            nc.vector.tensor_tensor(out=msq[:], in0=mean0[:], in1=mean0[:], op=ALU.mult)
             var = two.tile([P, 12], F32, tag="var")
-            nc.gpsimd.tensor_tensor(out=var[:], in0=e2[:], in1=msq[:], op=ALU.subtract)
-            varc = two.tile([P, 12], F32, tag="varc")
-            nc.gpsimd.tensor_scalar(
-                out=varc[:], in0=var[:], scalar1=3.0e38, scalar2=EPS_STD, op0=ALU.min, op1=ALU.max
+            nc.vector.scalar_tensor_tensor(
+                out=var[:], in0=s2[:], scalar=rtot[:, b : b + 1], in1=msq[:],
+                op0=ALU.mult, op1=ALU.subtract,
             )
+            varc = two.tile([P, 12], F32, tag="varc")
+            nc.vector.tensor_scalar_max(out=varc[:], in0=var[:], scalar1=EPS_STD)
             nc.gpsimd.tensor_tensor(
                 out=sin[:, 3:6, b, :],
                 in0=varc[:].rearrange("p (g j) -> p g j", j=4),
                 in1=half[:].rearrange("p (g j) -> p g j", j=4),
                 op=ALU.pow,
+            )
+            nc.vector.tensor_copy(
+                out=sin[:, 0:3, b, :], in_=mean0[:].rearrange("p (g j) -> p g j", j=4)
             )
 
         def qs(b):
@@ -280,21 +268,16 @@ def tile_attentivestatspool_pa_kernel(tc, x, mask, w1, b1, g1, be1, out):
                             ps1[:, P * ht : P * ht + P], u[:, ht, P * tb : P * tb + P], ident_f[:]
                         )
                     nc.vector.bn_stats(out=lst[:, i, :], in_=ps1[:])
-                    pbanks.append(ps1)
-                for i in range(2):
                     nc.vector.bn_aggr(out=mv[:, i, :], in_=lst[:, i, :])
+                    pbanks.append(ps1)
                 ve = four.tile([P, 2], F32, tag="ve")
-                nc.gpsimd.tensor_scalar(
-                    out=ve[:], in0=mv[:, :, 1], scalar1=EPS_LN, scalar2=1.0, op0=ALU.add, op1=ALU.mult
-                )
+                nc.vector.tensor_scalar_add(out=ve[:], in0=mv[:, :, 1], scalar1=EPS_LN)
+                nm = four.tile([P, 2], F32, tag="nm")
+                nc.vector.tensor_scalar_mul(out=nm[:], in0=mv[:, :, 0], scalar1=-1.0)
                 rstd = four.tile([P, 2], F32, tag="rstd")
                 nc.gpsimd.tensor_tensor(out=rstd[:], in0=ve[:], in1=mhalf[:, 0:2], op=ALU.pow)
-                nm = four.tile([P, 2], F32, tag="nm")
-                nc.gpsimd.tensor_tensor(out=nm[:], in0=mv[:, :, 0], in1=rstd[:], op=ALU.mult)
                 nb = four.tile([P, 2], F32, tag="nb")
-                nc.gpsimd.tensor_scalar(
-                    out=nb[:], in0=nm[:], scalar1=-1.0, scalar2=0.0, op0=ALU.mult, op1=ALU.add
-                )
+                nc.gpsimd.tensor_tensor(out=nb[:], in0=nm[:], in1=rstd[:], op=ALU.mult)
                 for i in range(2):
                     nc.scalar.activation(
                         out=zn[:, 2 * pair + i, :], in_=pbanks[i][:], func=ACT.Identity,
@@ -313,23 +296,12 @@ def tile_attentivestatspool_pa_kernel(tc, x, mask, w1, b1, g1, be1, out):
                 )
                 nc.sync.dma_start(out=out[b, P * ht : P * ht + P, :], in_=o[:])
 
-        units = [(b, g) for b in range(B) for g in range(3)]
-
-        def s_unit(k):
-            if k + 1 < len(units):
-                mask_unit(units[k + 1][0], units[k + 1][1])
-            bn_unit(units[k][0], units[k][1])
-
-        mask_unit(0, 0)
         for g in range(3):
             rg(0, g)
-        s_unit(0)
-        s_unit(1)
-        nc.vector.tensor_copy(out=prm_t[:], in_=prm_ps[:, 0:12])
+            s_unit(0, g)
+        xts.append(load_x(2))
         nc.vector.reciprocal(out=rtot[:], in_=tot[:])
         nc.vector.tensor_scalar_mul(out=c256[:], in0=rtot[:], scalar1=256.0)
-        s_unit(2)
-        xts.append(load_x(2))
         a_step(0)
         for g in range(9):
             wt_unit(g)
@@ -338,12 +310,15 @@ def tile_attentivestatspool_pa_kernel(tc, x, mask, w1, b1, g1, be1, out):
                 xts.append(load_x(3))
         for g in range(3):
             qx(0, g)
+        prm_ps = ps_b.tile([P, P], BF16, tag="mm")
+        nc.tensor.transpose(prm_ps[:], prm[:], ident_b[:])
+        nc.vector.tensor_copy(out=prm_t[:], in_=prm_ps[:, 0:12])
         qs(0)
         main(0)
         for b in range(1, B):
             for g in range(3):
                 rg(b, g)
-                s_unit(3 * b + g)
+                s_unit(b, g)
                 if b == 3 and g == 0:
                     layer_norm(1)
             if b == 2:

@@ -14,6 +14,14 @@ AX = mybir.AxisListType
 
 B, C, T, H = 4, 1536, 512, 512
 P = 128
+SLOTS = 4
+K_PASS = P * SLOTS
+X_PASSES = C // K_PASS
+W_PASSES = 3 * X_PASSES
+ROWS = X_PASSES * SLOTS
+H_TILES = H // P
+T_TILES = T // P
+STAT_STEP = 64
 EPS_LN = 1e-5
 EPS_STD = 1e-5
 FLOPS = 2 * B * H * 3 * C * T
@@ -23,311 +31,324 @@ def tile_attentivestatspool_pa_kernel(tc, x, mask, w1, b1, g1, be1, out):
     nc = tc.nc
     with ExitStack() as ctx:
         const = ctx.enter_context(tc.tile_pool(name="const", bufs=1))
-        big = ctx.enter_context(tc.tile_pool(name="big", bufs=5))
-        work = ctx.enter_context(tc.tile_pool(name="work", bufs=3))
+        loads = ctx.enter_context(tc.tile_pool(name="loads", bufs=5))
+        three = ctx.enter_context(tc.tile_pool(name="three", bufs=3))
         four = ctx.enter_context(tc.tile_pool(name="four", bufs=4))
         two = ctx.enter_context(tc.tile_pool(name="two", bufs=2))
-        outp = ctx.enter_context(tc.tile_pool(name="outp", bufs=4))
-        ps_a = ctx.enter_context(tc.psum_pool(name="ps_a", bufs=4))
-        ps_b = ctx.enter_context(tc.psum_pool(name="ps_b", bufs=2))
-        ps_c = ctx.enter_context(tc.psum_pool(name="ps_c", bufs=2))
+        ps_first = ctx.enter_context(tc.psum_pool(name="ps_first", bufs=4))
+        ps_mx = ctx.enter_context(tc.psum_pool(name="ps_mx", bufs=2))
+        ps_back = ctx.enter_context(tc.psum_pool(name="ps_back", bufs=2))
 
-        mrow = const.tile([P, B * T], BF16)
-        nc.vector.memset(mrow[:], 0.0)
-        nc.sync.dma_start(out=mrow[0:1, :], in_=mask.rearrange("b o t -> o (b t)"))
+        mask_row = const.tile([P, B * T], BF16)
+        nc.vector.memset(mask_row[:], 0.0)
+        nc.sync.dma_start(out=mask_row[0:1, :], in_=mask.rearrange("b o t -> o (b t)"))
         ones = const.tile([P, P], BF16)
         nc.vector.memset(ones[:], 1.0)
-        maskb = const.tile([P, B, T], BF16)
-        tot = const.tile([P, B], F32)
-        prm = const.tile([P, P], BF16)
-        nc.vector.memset(prm[:], 0.0)
+        mask_all = const.tile([P, B, T], BF16)
+        mask_sum = const.tile([P, B], F32)
+        param_rows = const.tile([P, P], BF16)
+        nc.vector.memset(param_rows[:], 0.0)
         warm = const.tile([P, 1], F32)
         nc.vector.memset(warm[:], 0.0)
         nc.scalar.activation(out=warm[:], in_=warm[:], func=ACT.Tanh)
 
         def load_x(b):
-            xt = big.tile([P, 12, T], BF16, tag="big", name="xt%d" % b)
-            for g in range(3):
+            x_tile = loads.tile([P, ROWS, T], BF16, tag="load", name="x_tile%d" % b)
+            for g in range(X_PASSES):
                 nc.sync.dma_start(
-                    out=xt[:, 4 * g : 4 * g + 4, :].rearrange("p (u e) t -> p u (e t)", u=2),
-                    in_=x[b, 512 * g : 512 * (g + 1), :].rearrange(
+                    out=x_tile[:, SLOTS * g : SLOTS * (g + 1), :].rearrange(
+                        "p (u e) t -> p u (e t)", u=2
+                    ),
+                    in_=x[b, K_PASS * g : K_PASS * (g + 1), :].rearrange(
                         "(u p e) t -> p u (e t)", u=2, p=P, e=2
                     ),
                 )
-            return xt
+            return x_tile
 
-        def load_w(kc):
-            wt = big.tile([P, 4, C], BF16, tag="big", name="wt%d" % kc)
+        def load_w(third):
+            w_tile = loads.tile([P, H_TILES, C], BF16, tag="load", name="w_tile%d" % third)
             nc.sync.dma_start(
-                out=wt[:],
-                in_=w1[:, C * kc : C * (kc + 1)].rearrange("(a p) k -> p a k", p=P),
+                out=w_tile[:],
+                in_=w1[:, C * third : C * (third + 1)].rearrange("(a p) k -> p a k", p=P),
             )
-            return wt
+            return w_tile
 
-        xts = [load_x(0)]
-        wts = [load_w(kc) for kc in range(3)]
-        xts.append(load_x(1))
-        nc.sync.dma_start(out=prm[0:4, :], in_=b1.rearrange("(r c) -> r c", c=P))
-        nc.sync.dma_start(out=prm[4:8, :], in_=g1.rearrange("(r c) -> r c", c=P))
-        nc.sync.dma_start(out=prm[8:12, :], in_=be1.rearrange("(r c) -> r c", c=P))
+        x_tiles = [load_x(0)]
+        w_tiles = [load_w(third) for third in range(3)]
+        x_tiles.append(load_x(1))
+        nc.sync.dma_start(out=param_rows[0:4, :], in_=b1.rearrange("(r c) -> r c", c=P))
+        nc.sync.dma_start(out=param_rows[4:8, :], in_=g1.rearrange("(r c) -> r c", c=P))
+        nc.sync.dma_start(out=param_rows[8:12, :], in_=be1.rearrange("(r c) -> r c", c=P))
 
-        ident_f = const.tile([P, P], F32)
-        make_identity(nc, ident_f[:])
-        ident_b = const.tile([P, P], BF16)
-        make_identity(nc, ident_b[:])
-        sin = const.tile([P, 8, 64, 4], BF16, align_bytes=64)
-        nc.vector.memset(sin[:], 0.0)
-        half = const.tile([P, 12], F32)
+        ident_f32 = const.tile([P, P], F32)
+        make_identity(nc, ident_f32[:])
+        ident_bf16 = const.tile([P, P], BF16)
+        make_identity(nc, ident_bf16[:])
+        stat_in = const.tile([P, 8, STAT_STEP, SLOTS], BF16, align_bytes=64)
+        nc.vector.memset(stat_in[:], 0.0)
+        half = const.tile([P, ROWS], F32)
         nc.vector.memset(half[:], 0.5)
-        mhalf = const.tile([P, 4], F32)
-        nc.vector.memset(mhalf[:], -0.5)
+        minus_half = const.tile([P, 4], F32)
+        nc.vector.memset(minus_half[:], -0.5)
 
-        wq = const.tile([P, 9, H], U32, align_bytes=64)
-        wsc = const.tile([P, 9, H], U8, align_bytes=64)
+        w_codes = const.tile([P, W_PASSES, H], U32, align_bytes=64)
+        w_scales = const.tile([P, W_PASSES, H], U8, align_bytes=64)
 
         for b in range(B):
-            m_ps = ps_b.tile([P, T], F32, tag="mm")
+            mask_ps = ps_mx.tile([P, T], F32, tag="mx")
             nc.tensor.matmul(
-                out=m_ps[:], lhsT=ones[:], rhs=mrow[:, T * b : T * (b + 1)], start=True, stop=True
+                out=mask_ps[:], lhsT=ones[:], rhs=mask_row[:, T * b : T * (b + 1)],
+                start=True, stop=True,
             )
             nc.scalar.activation(
-                out=maskb[:, b, :], in_=m_ps[:], func=ACT.Copy, accum_out=tot[:, b : b + 1]
+                out=mask_all[:, b, :], in_=mask_ps[:], func=ACT.Copy,
+                accum_out=mask_sum[:, b : b + 1],
             )
-        rtot = const.tile([P, B], F32)
-        c256 = const.tile([P, B], F32)
+        inv_sum = const.tile([P, B], F32)
+        inv_sum_256 = const.tile([P, B], F32)
+        params = const.tile([P, 12], F32)
 
-        prm_t = const.tile([P, 12], F32)
+        stats = {}
+        x_grouped = {}
+        x_quant = {}
+        w_grouped = {}
+        stat_ps = {}
+        relu_out = {}
 
-        sts = {}
-        xgs = {}
-        xqs = {}
-        wgs = {}
-        sqs = {}
-        biases = {}
-        us = {}
-
-        def s_unit(b, g):
+        def masked_stats(b, g):
             if g == 0:
-                st_new = two.tile([P, 12, 6], F32, tag="st")
-                sts[b] = st_new
-            xm = two.tile([P, 4, T], BF16, tag="xm")
+                stats_b = two.tile([P, ROWS, 6], F32, tag="stats")
+                stats[b] = stats_b
+            x_masked = two.tile([P, SLOTS, T], BF16, tag="x_masked")
             nc.vector.tensor_tensor(
-                out=xm[:],
-                in0=xts[b][:, 4 * g : 4 * g + 4, :],
-                in1=maskb[:, b, :].unsqueeze(1).to_broadcast([P, 4, T]),
+                out=x_masked[:],
+                in0=x_tiles[b][:, SLOTS * g : SLOTS * (g + 1), :],
+                in1=mask_all[:, b, :].unsqueeze(1).to_broadcast([P, SLOTS, T]),
                 op=ALU.mult,
             )
-            for j in range(4):
-                nc.vector.bn_stats(out=sts[b][:, 4 * g + j, :], in_=xm[:, j, :])
+            for j in range(SLOTS):
+                nc.vector.bn_stats(out=stats[b][:, SLOTS * g + j, :], in_=x_masked[:, j, :])
 
-        def wt_unit(g):
-            kc, gl = divmod(g, 3)
-            w32 = wts[kc][:].bitcast(F32)
-            wg = four.tile([P, H, 4], BF16, tag="wg", align_bytes=64)
-            wgs[g] = wg
-            wg32 = wg[:].bitcast(F32)
-            for a2 in range(2):
-                wps = ps_a.tile([P, 2, 256], F32, tag="t1")
+        def transpose_w(g):
+            third, g_in = divmod(g, X_PASSES)
+            w_words = w_tiles[third][:].bitcast(F32)
+            w_group = four.tile([P, H, SLOTS], BF16, tag="w_group", align_bytes=64)
+            w_grouped[g] = w_group
+            group_words = w_group[:].bitcast(F32)
+            for pair in range(2):
+                w_ps = ps_first.tile([P, 2, 2 * P], F32, tag="first")
                 for u in range(2):
                     for a in range(2):
-                        c0 = 256 * gl + 128 * u
+                        first_word = 2 * P * g_in + P * u
                         nc.tensor.transpose(
-                            wps[:, u, 128 * a : 128 * a + 128],
-                            w32[:, 2 * a2 + a, c0 : c0 + 128],
-                            ident_f[:],
+                            w_ps[:, u, P * a : P * (a + 1)],
+                            w_words[:, 2 * pair + a, first_word : first_word + P],
+                            ident_f32[:],
                         )
                 nc.scalar.copy(
-                    out=wg32[:, 256 * a2 : 256 * a2 + 256, :],
-                    in_=wps[:].rearrange("p u n -> p n u"),
+                    out=group_words[:, 2 * P * pair : 2 * P * (pair + 1), :],
+                    in_=w_ps[:].rearrange("p u n -> p n u"),
                 )
 
-        def qw(g):
+        def quantise_w(g):
             nc.vector.quantize_mx(
-                out=wq[:, g, :].bitcast(FP8X4),
-                scales=wsc[:, g, :],
-                in_=wgs[g][:].rearrange("p h j -> p (h j)"),
+                out=w_codes[:, g, :].bitcast(FP8X4),
+                scales=w_scales[:, g, :],
+                in_=w_grouped[g][:].rearrange("p h j -> p (h j)"),
             )
 
-        def rg(b, g):
-            xg = work.tile([P, T, 4], BF16, tag="xg", align_bytes=64)
-            xgs[(b, g)] = xg
+        def group_x(b, g):
+            x_group = three.tile([P, T, SLOTS], BF16, tag="x_group", align_bytes=64)
+            x_grouped[(b, g)] = x_group
             nc.scalar.copy(
-                out=xg[:].rearrange("p (c i) j -> p c j i", i=4),
-                in_=xts[b][:, 4 * g : 4 * g + 4, :].rearrange("p j (c i) -> p c j i", i=4),
+                out=x_group[:].rearrange("p (c i) j -> p c j i", i=4),
+                in_=x_tiles[b][:, SLOTS * g : SLOTS * (g + 1), :].rearrange(
+                    "p j (c i) -> p c j i", i=4
+                ),
             )
 
-        def qx(b, g):
+        def quantise_x(b, g):
             if g == 0:
-                xq_new = work.tile([P, 3, T], U32, tag="xq", align_bytes=64)
-                xsc_new = work.tile([P, 3, T], U8, tag="xsc", align_bytes=64)
-                xqs[b] = (xq_new, xsc_new)
-            xq, xsc = xqs[b]
+                x_codes = three.tile([P, X_PASSES, T], U32, tag="x_codes", align_bytes=64)
+                x_scales = three.tile([P, X_PASSES, T], U8, tag="x_scales", align_bytes=64)
+                x_quant[b] = (x_codes, x_scales)
+            x_codes, x_scales = x_quant[b]
             nc.vector.quantize_mx(
-                out=xq[:, g, :].bitcast(FP8X4),
-                scales=xsc[:, g, :],
-                in_=xgs[(b, g)][:].rearrange("p t j -> p (t j)"),
+                out=x_codes[:, g, :].bitcast(FP8X4),
+                scales=x_scales[:, g, :],
+                in_=x_grouped[(b, g)][:].rearrange("p t j -> p (t j)"),
             )
 
-        def a_step(b):
-            stv = sts[b][:].rearrange("p r (h s) -> p (r h) s", s=3)
-            mcol = stv[:, :, 1]
-            vcol = stv[:, :, 2]
-            sq = two.tile([P, 24], F32, tag="sq")
-            nc.vector.tensor_tensor(out=sq[:], in0=mcol, in1=mcol, op=ALU.mult)
-            t2 = two.tile([P, 24], F32, tag="t2")
+        def mean_and_std(b):
+            halves = stats[b][:].rearrange("p r (h s) -> p (r h) s", s=3)
+            half_mean = halves[:, :, 1]
+            half_dev = halves[:, :, 2]
+            mean_sq = two.tile([P, 2 * ROWS], F32, tag="mean_sq")
+            nc.vector.tensor_tensor(out=mean_sq[:], in0=half_mean, in1=half_mean, op=ALU.mult)
+            half_sq = two.tile([P, 2 * ROWS], F32, tag="half_sq")
             nc.vector.scalar_tensor_tensor(
-                out=t2[:], in0=sq[:], scalar=256.0, in1=vcol, op0=ALU.mult, op1=ALU.add
+                out=half_sq[:], in0=mean_sq[:], scalar=256.0, in1=half_dev,
+                op0=ALU.mult, op1=ALU.add,
             )
-            s2 = two.tile([P, 12], F32, tag="s2")
+            sum_sq = two.tile([P, ROWS], F32, tag="sum_sq")
             nc.vector.tensor_reduce(
-                out=s2[:], in_=t2[:].rearrange("p (r h) -> p r h", h=2), axis=AX.X, op=ALU.add
+                out=sum_sq[:], in_=half_sq[:].rearrange("p (r h) -> p r h", h=2),
+                axis=AX.X, op=ALU.add,
             )
-            s1 = two.tile([P, 12], F32, tag="s1")
+            sum_mean = two.tile([P, ROWS], F32, tag="sum_mean")
             nc.vector.tensor_reduce(
-                out=s1[:], in_=mcol.rearrange("p (r h) -> p r h", h=2), axis=AX.X, op=ALU.add
+                out=sum_mean[:], in_=half_mean.rearrange("p (r h) -> p r h", h=2),
+                axis=AX.X, op=ALU.add,
             )
-            mean0 = two.tile([P, 12], F32, tag="mean0")
-            nc.vector.tensor_scalar_mul(out=mean0[:], in0=s1[:], scalar1=c256[:, b : b + 1])
-            msq = two.tile([P, 12], F32, tag="msq")
-            nc.vector.tensor_tensor(out=msq[:], in0=mean0[:], in1=mean0[:], op=ALU.mult)
-            var = two.tile([P, 12], F32, tag="var")
+            mean0 = two.tile([P, ROWS], F32, tag="mean0")
+            nc.vector.tensor_scalar_mul(
+                out=mean0[:], in0=sum_mean[:], scalar1=inv_sum_256[:, b : b + 1]
+            )
+            mean0_sq = two.tile([P, ROWS], F32, tag="mean0_sq")
+            nc.vector.tensor_tensor(out=mean0_sq[:], in0=mean0[:], in1=mean0[:], op=ALU.mult)
+            var0 = two.tile([P, ROWS], F32, tag="var0")
             nc.vector.scalar_tensor_tensor(
-                out=var[:], in0=s2[:], scalar=rtot[:, b : b + 1], in1=msq[:],
+                out=var0[:], in0=sum_sq[:], scalar=inv_sum[:, b : b + 1], in1=mean0_sq[:],
                 op0=ALU.mult, op1=ALU.subtract,
             )
-            varc = two.tile([P, 12], F32, tag="varc")
-            nc.vector.tensor_scalar_max(out=varc[:], in0=var[:], scalar1=EPS_STD)
+            var0_floor = two.tile([P, ROWS], F32, tag="var0_floor")
+            nc.vector.tensor_scalar_max(out=var0_floor[:], in0=var0[:], scalar1=EPS_STD)
             nc.gpsimd.tensor_tensor(
-                out=sin[:, 3:6, b, :],
-                in0=varc[:].rearrange("p (g j) -> p g j", j=4),
-                in1=half[:].rearrange("p (g j) -> p g j", j=4),
+                out=stat_in[:, X_PASSES : 2 * X_PASSES, b, :],
+                in0=var0_floor[:].rearrange("p (g j) -> p g j", j=SLOTS),
+                in1=half[:].rearrange("p (g j) -> p g j", j=SLOTS),
                 op=ALU.pow,
             )
             nc.vector.tensor_copy(
-                out=sin[:, 0:3, b, :], in_=mean0[:].rearrange("p (g j) -> p g j", j=4)
+                out=stat_in[:, 0:X_PASSES, b, :],
+                in_=mean0[:].rearrange("p (g j) -> p g j", j=SLOTS),
             )
 
-        def qs(b):
-            sqt = two.tile([P, 512], U32, tag="sqt", align_bytes=64)
-            ssc = two.tile([P, 512], U8, tag="ssc", align_bytes=64)
+        def stat_product(b):
+            stat_codes = two.tile([P, 8 * STAT_STEP], U32, tag="stat_codes", align_bytes=64)
+            stat_scales = two.tile([P, 8 * STAT_STEP], U8, tag="stat_scales", align_bytes=64)
             nc.vector.quantize_mx(
-                out=sqt[:].bitcast(FP8X4),
-                scales=ssc[:],
-                in_=sin[:].rearrange("p s n j -> p (s n j)"),
+                out=stat_codes[:].bitcast(FP8X4),
+                scales=stat_scales[:],
+                in_=stat_in[:].rearrange("p s n j -> p (s n j)"),
             )
-            ps_s = ps_b.tile([P, 4, P], F32, tag="mm")
-            sqs[b] = ps_s
-            for ht in range(4):
-                for s in range(6):
+            product = ps_mx.tile([P, H_TILES, P], F32, tag="mx")
+            stat_ps[b] = product
+            for ht in range(H_TILES):
+                for s in range(2 * X_PASSES):
                     nc.tensor.matmul_mx(
-                        out=ps_s[:, ht, :],
-                        lhsT=wq[:, 3 + s, P * ht : P * ht + P].bitcast(FP8X4),
-                        lhsT_scale=wsc[:, 3 + s, P * ht : P * ht + P],
-                        rhs=sqt[:, 64 * s : 64 * s + P].bitcast(FP8X4),
-                        rhs_scale=ssc[:, 64 * s : 64 * s + P],
+                        out=product[:, ht, :],
+                        lhsT=w_codes[:, X_PASSES + s, P * ht : P * (ht + 1)].bitcast(FP8X4),
+                        lhsT_scale=w_scales[:, X_PASSES + s, P * ht : P * (ht + 1)],
+                        rhs=stat_codes[:, STAT_STEP * s : STAT_STEP * s + P].bitcast(FP8X4),
+                        rhs_scale=stat_scales[:, STAT_STEP * s : STAT_STEP * s + P],
                         start=(s == 0),
-                        stop=(s == 5),
+                        stop=(s == 2 * X_PASSES - 1),
                     )
 
-        def main(b):
-            bias = two.tile([P, 4], F32, tag="bias")
+        def main_product(b):
+            bias = two.tile([P, H_TILES], F32, tag="bias")
             nc.vector.tensor_tensor(
-                out=bias[:], in0=sqs[b][:, :, b], in1=prm_t[:, 0:4], op=ALU.add
+                out=bias[:], in0=stat_ps[b][:, :, b], in1=params[:, 0:4], op=ALU.add
             )
-            xq, xsc = xqs[b]
-            u = work.tile([P, 4, T], F32, tag="u")
-            us[b] = u
-            for ht in range(4):
-                ps_m = ps_b.tile([P, T], F32, tag="mm")
-                for g in range(3):
+            x_codes, x_scales = x_quant[b]
+            u = three.tile([P, H_TILES, T], F32, tag="u")
+            relu_out[b] = u
+            for ht in range(H_TILES):
+                acc = ps_mx.tile([P, T], F32, tag="mx")
+                for g in range(X_PASSES):
                     nc.tensor.matmul_mx(
-                        out=ps_m[:],
-                        lhsT=wq[:, g, P * ht : P * ht + P].bitcast(FP8X4),
-                        lhsT_scale=wsc[:, g, P * ht : P * ht + P],
-                        rhs=xq[:, g, :].bitcast(FP8X4),
-                        rhs_scale=xsc[:, g, :],
+                        out=acc[:],
+                        lhsT=w_codes[:, g, P * ht : P * (ht + 1)].bitcast(FP8X4),
+                        lhsT_scale=w_scales[:, g, P * ht : P * (ht + 1)],
+                        rhs=x_codes[:, g, :].bitcast(FP8X4),
+                        rhs_scale=x_scales[:, g, :],
                         start=(g == 0),
-                        stop=(g == 2),
+                        stop=(g == X_PASSES - 1),
                     )
                 nc.scalar.activation(
-                    out=u[:, ht, :], in_=ps_m[:], func=ACT.Relu, bias=bias[:, ht : ht + 1], scale=1.0
+                    out=u[:, ht, :], in_=acc[:], func=ACT.Relu, bias=bias[:, ht : ht + 1], scale=1.0
                 )
 
         def layer_norm(b):
-            u = us[b]
-            zn = two.tile([P, 4, H], F32, tag="zn")
+            u = relu_out[b]
+            normed = two.tile([P, T_TILES, H], F32, tag="normed")
             for pair in range(2):
-                lst = four.tile([P, 2, 6], F32, tag="lst")
-                mv = four.tile([P, 2, 2], F32, tag="mv")
-                pbanks = []
+                ln_stats = four.tile([P, 2, 6], F32, tag="ln_stats")
+                mean_var = four.tile([P, 2, 2], F32, tag="mean_var")
+                banks = []
                 for i in range(2):
                     tb = 2 * pair + i
-                    ps1 = ps_a.tile([P, H], F32, tag="t1")
-                    for ht in range(4):
+                    u_t = ps_first.tile([P, H], F32, tag="first")
+                    for ht in range(H_TILES):
                         nc.tensor.transpose(
-                            ps1[:, P * ht : P * ht + P], u[:, ht, P * tb : P * tb + P], ident_f[:]
+                            u_t[:, P * ht : P * (ht + 1)], u[:, ht, P * tb : P * (tb + 1)],
+                            ident_f32[:],
                         )
-                    nc.vector.bn_stats(out=lst[:, i, :], in_=ps1[:])
-                    nc.vector.bn_aggr(out=mv[:, i, :], in_=lst[:, i, :])
-                    pbanks.append(ps1)
-                ve = four.tile([P, 2], F32, tag="ve")
-                nc.vector.tensor_scalar_add(out=ve[:], in0=mv[:, :, 1], scalar1=EPS_LN)
-                nm = four.tile([P, 2], F32, tag="nm")
-                nc.vector.tensor_scalar_mul(out=nm[:], in0=mv[:, :, 0], scalar1=-1.0)
+                    nc.vector.bn_stats(out=ln_stats[:, i, :], in_=u_t[:])
+                    nc.vector.bn_aggr(out=mean_var[:, i, :], in_=ln_stats[:, i, :])
+                    banks.append(u_t)
+                var_eps = four.tile([P, 2], F32, tag="var_eps")
+                nc.vector.tensor_scalar_add(out=var_eps[:], in0=mean_var[:, :, 1], scalar1=EPS_LN)
+                neg_mean = four.tile([P, 2], F32, tag="neg_mean")
+                nc.vector.tensor_scalar_mul(out=neg_mean[:], in0=mean_var[:, :, 0], scalar1=-1.0)
                 rstd = four.tile([P, 2], F32, tag="rstd")
-                nc.gpsimd.tensor_tensor(out=rstd[:], in0=ve[:], in1=mhalf[:, 0:2], op=ALU.pow)
-                nb = four.tile([P, 2], F32, tag="nb")
-                nc.gpsimd.tensor_tensor(out=nb[:], in0=nm[:], in1=rstd[:], op=ALU.mult)
+                nc.gpsimd.tensor_tensor(
+                    out=rstd[:], in0=var_eps[:], in1=minus_half[:, 0:2], op=ALU.pow
+                )
+                shift = four.tile([P, 2], F32, tag="shift")
+                nc.gpsimd.tensor_tensor(out=shift[:], in0=neg_mean[:], in1=rstd[:], op=ALU.mult)
                 for i in range(2):
                     nc.scalar.activation(
-                        out=zn[:, 2 * pair + i, :], in_=pbanks[i][:], func=ACT.Identity,
-                        scale=rstd[:, i : i + 1], bias=nb[:, i : i + 1],
+                        out=normed[:, 2 * pair + i, :], in_=banks[i][:], func=ACT.Identity,
+                        scale=rstd[:, i : i + 1], bias=shift[:, i : i + 1],
                     )
-            for ht in range(4):
-                ps2 = ps_c.tile([P, T], F32, tag="t2")
-                for tb in range(4):
+            for ht in range(H_TILES):
+                back = ps_back.tile([P, T], F32, tag="back")
+                for tb in range(T_TILES):
                     nc.tensor.transpose(
-                        ps2[:, P * tb : P * tb + P], zn[:, tb, P * ht : P * ht + P], ident_f[:]
+                        back[:, P * tb : P * (tb + 1)], normed[:, tb, P * ht : P * (ht + 1)],
+                        ident_f32[:],
                     )
-                o = outp.tile([P, T], F32, tag="o")
+                result = four.tile([P, T], F32, tag="result")
                 nc.scalar.activation(
-                    out=o[:], in_=ps2[:], func=ACT.Tanh,
-                    scale=prm_t[:, 4 + ht : 5 + ht], bias=prm_t[:, 8 + ht : 9 + ht],
+                    out=result[:], in_=back[:], func=ACT.Tanh,
+                    scale=params[:, 4 + ht : 5 + ht], bias=params[:, 8 + ht : 9 + ht],
                 )
-                nc.sync.dma_start(out=out[b, P * ht : P * ht + P, :], in_=o[:])
+                nc.sync.dma_start(out=out[b, P * ht : P * (ht + 1), :], in_=result[:])
 
-        for g in range(3):
-            rg(0, g)
-            s_unit(0, g)
-        xts.append(load_x(2))
-        nc.vector.reciprocal(out=rtot[:], in_=tot[:])
-        nc.vector.tensor_scalar_mul(out=c256[:], in0=rtot[:], scalar1=256.0)
-        a_step(0)
-        for g in range(9):
-            wt_unit(g)
-            qw(g)
-            if g == 2:
-                xts.append(load_x(3))
-        for g in range(3):
-            qx(0, g)
-        prm_ps = ps_b.tile([P, P], BF16, tag="mm")
-        nc.tensor.transpose(prm_ps[:], prm[:], ident_b[:])
-        nc.vector.tensor_copy(out=prm_t[:], in_=prm_ps[:, 0:12])
-        qs(0)
-        main(0)
+        for g in range(X_PASSES):
+            group_x(0, g)
+            masked_stats(0, g)
+        x_tiles.append(load_x(2))
+        nc.vector.reciprocal(out=inv_sum[:], in_=mask_sum[:])
+        nc.vector.tensor_scalar_mul(out=inv_sum_256[:], in0=inv_sum[:], scalar1=256.0)
+        mean_and_std(0)
+        for g in range(W_PASSES):
+            transpose_w(g)
+            quantise_w(g)
+            if g == X_PASSES - 1:
+                x_tiles.append(load_x(3))
+        for g in range(X_PASSES):
+            quantise_x(0, g)
+        param_ps = ps_mx.tile([P, P], BF16, tag="mx")
+        nc.tensor.transpose(param_ps[:], param_rows[:], ident_bf16[:])
+        nc.vector.tensor_copy(out=params[:], in_=param_ps[:, 0:12])
+        stat_product(0)
+        main_product(0)
         for b in range(1, B):
-            for g in range(3):
-                rg(b, g)
-                s_unit(b, g)
+            for g in range(X_PASSES):
+                group_x(b, g)
+                masked_stats(b, g)
                 if b == 3 and g == 0:
                     layer_norm(1)
             if b == 2:
                 layer_norm(0)
-            a_step(b)
-            for g in range(3):
-                qx(b, g)
-            qs(b)
+            mean_and_std(b)
+            for g in range(X_PASSES):
+                quantise_x(b, g)
+            stat_product(b)
             if b == 3:
                 layer_norm(2)
-            main(b)
+            main_product(b)
         layer_norm(3)

from contextlib import ExitStack

import concourse.mybir as mybir
from concourse.masks import make_identity

F32 = mybir.dt.float32
BF16 = mybir.dt.bfloat16
U32 = mybir.dt.uint32
U8 = mybir.dt.uint8
FP8X4 = mybir.dt.float8_e4m3fn_x4
ALU = mybir.AluOpType
ACT = mybir.ActivationFunctionType
AX = mybir.AxisListType

B, C, T, H = 4, 1536, 512, 512
P = 128
SLOTS = 4
K_PASS = P * SLOTS
X_PASSES = C // K_PASS
W_PASSES = 3 * X_PASSES
ROWS = X_PASSES * SLOTS
H_TILES = H // P
T_TILES = T // P
STAT_STEP = 64
EPS_LN = 1e-5
EPS_STD = 1e-5
FLOPS = 2 * B * H * 3 * C * T


def tile_attentivestatspool_pa_kernel(tc, x, mask, w1, b1, g1, be1, out):
    nc = tc.nc
    with ExitStack() as ctx:
        const = ctx.enter_context(tc.tile_pool(name="const", bufs=1))
        loads = ctx.enter_context(tc.tile_pool(name="loads", bufs=5))
        three = ctx.enter_context(tc.tile_pool(name="three", bufs=3))
        four = ctx.enter_context(tc.tile_pool(name="four", bufs=4))
        two = ctx.enter_context(tc.tile_pool(name="two", bufs=2))
        ps_first = ctx.enter_context(tc.psum_pool(name="ps_first", bufs=4))
        ps_mx = ctx.enter_context(tc.psum_pool(name="ps_mx", bufs=2))
        ps_back = ctx.enter_context(tc.psum_pool(name="ps_back", bufs=2))

        mask_row = const.tile([P, B * T], BF16)
        nc.vector.memset(mask_row[:], 0.0)
        nc.sync.dma_start(out=mask_row[0:1, :], in_=mask.rearrange("b o t -> o (b t)"))
        ones = const.tile([P, P], BF16)
        nc.vector.memset(ones[:], 1.0)
        mask_all = const.tile([P, B, T], BF16)
        mask_sum = const.tile([P, B], F32)
        param_rows = const.tile([P, P], BF16)
        nc.vector.memset(param_rows[:], 0.0)
        warm = const.tile([P, 1], F32)
        nc.vector.memset(warm[:], 0.0)
        nc.scalar.activation(out=warm[:], in_=warm[:], func=ACT.Tanh)

        def load_x(b):
            x_tile = loads.tile([P, ROWS, T], BF16, tag="load", name="x_tile%d" % b)
            for g in range(X_PASSES):
                nc.sync.dma_start(
                    out=x_tile[:, SLOTS * g : SLOTS * (g + 1), :].rearrange(
                        "p (u e) t -> p u (e t)", u=2
                    ),
                    in_=x[b, K_PASS * g : K_PASS * (g + 1), :].rearrange(
                        "(u p e) t -> p u (e t)", u=2, p=P, e=2
                    ),
                )
            return x_tile

        def load_w(third):
            w_tile = loads.tile([P, H_TILES, C], BF16, tag="load", name="w_tile%d" % third)
            nc.sync.dma_start(
                out=w_tile[:],
                in_=w1[:, C * third : C * (third + 1)].rearrange("(a p) k -> p a k", p=P),
            )
            return w_tile

        x_tiles = [load_x(0)]
        w_tiles = [load_w(third) for third in range(3)]
        x_tiles.append(load_x(1))
        nc.sync.dma_start(out=param_rows[0:4, :], in_=b1.rearrange("(r c) -> r c", c=P))
        nc.sync.dma_start(out=param_rows[4:8, :], in_=g1.rearrange("(r c) -> r c", c=P))
        nc.sync.dma_start(out=param_rows[8:12, :], in_=be1.rearrange("(r c) -> r c", c=P))

        ident_f32 = const.tile([P, P], F32)
        make_identity(nc, ident_f32[:])
        ident_bf16 = const.tile([P, P], BF16)
        make_identity(nc, ident_bf16[:])
        stat_in = const.tile([P, 8, STAT_STEP, SLOTS], BF16, align_bytes=64)
        nc.vector.memset(stat_in[:], 0.0)
        half = const.tile([P, ROWS], F32)
        nc.vector.memset(half[:], 0.5)
        minus_half = const.tile([P, 4], F32)
        nc.vector.memset(minus_half[:], -0.5)

        w_codes = const.tile([P, W_PASSES, H], U32, align_bytes=64)
        w_scales = const.tile([P, W_PASSES, H], U8, align_bytes=64)

        for b in range(B):
            mask_ps = ps_mx.tile([P, T], F32, tag="mx")
            nc.tensor.matmul(
                out=mask_ps[:], lhsT=ones[:], rhs=mask_row[:, T * b : T * (b + 1)],
                start=True, stop=True,
            )
            nc.scalar.activation(
                out=mask_all[:, b, :], in_=mask_ps[:], func=ACT.Copy,
                accum_out=mask_sum[:, b : b + 1],
            )
        inv_sum = const.tile([P, B], F32)
        inv_sum_256 = const.tile([P, B], F32)
        params = const.tile([P, 12], F32)

        stats = {}
        x_grouped = {}
        x_quant = {}
        w_grouped = {}
        stat_ps = {}
        relu_out = {}

        def masked_stats(b, g):
            if g == 0:
                stats_b = two.tile([P, ROWS, 6], F32, tag="stats")
                stats[b] = stats_b
            x_masked = two.tile([P, SLOTS, T], BF16, tag="x_masked")
            nc.vector.tensor_tensor(
                out=x_masked[:],
                in0=x_tiles[b][:, SLOTS * g : SLOTS * (g + 1), :],
                in1=mask_all[:, b, :].unsqueeze(1).to_broadcast([P, SLOTS, T]),
                op=ALU.mult,
            )
            for j in range(SLOTS):
                nc.vector.bn_stats(out=stats[b][:, SLOTS * g + j, :], in_=x_masked[:, j, :])

        def transpose_w(g):
            third, g_in = divmod(g, X_PASSES)
            w_words = w_tiles[third][:].bitcast(F32)
            w_group = four.tile([P, H, SLOTS], BF16, tag="w_group", align_bytes=64)
            w_grouped[g] = w_group
            group_words = w_group[:].bitcast(F32)
            for pair in range(2):
                w_ps = ps_first.tile([P, 2, 2 * P], F32, tag="first")
                for u in range(2):
                    for a in range(2):
                        first_word = 2 * P * g_in + P * u
                        nc.tensor.transpose(
                            w_ps[:, u, P * a : P * (a + 1)],
                            w_words[:, 2 * pair + a, first_word : first_word + P],
                            ident_f32[:],
                        )
                nc.scalar.copy(
                    out=group_words[:, 2 * P * pair : 2 * P * (pair + 1), :],
                    in_=w_ps[:].rearrange("p u n -> p n u"),
                )

        def quantise_w(g):
            nc.vector.quantize_mx(
                out=w_codes[:, g, :].bitcast(FP8X4),
                scales=w_scales[:, g, :],
                in_=w_grouped[g][:].rearrange("p h j -> p (h j)"),
            )

        def group_x(b, g):
            x_group = three.tile([P, T, SLOTS], BF16, tag="x_group", align_bytes=64)
            x_grouped[(b, g)] = x_group
            nc.scalar.copy(
                out=x_group[:].rearrange("p (c i) j -> p c j i", i=4),
                in_=x_tiles[b][:, SLOTS * g : SLOTS * (g + 1), :].rearrange(
                    "p j (c i) -> p c j i", i=4
                ),
            )

        def quantise_x(b, g):
            if g == 0:
                x_codes = three.tile([P, X_PASSES, T], U32, tag="x_codes", align_bytes=64)
                x_scales = three.tile([P, X_PASSES, T], U8, tag="x_scales", align_bytes=64)
                x_quant[b] = (x_codes, x_scales)
            x_codes, x_scales = x_quant[b]
            nc.vector.quantize_mx(
                out=x_codes[:, g, :].bitcast(FP8X4),
                scales=x_scales[:, g, :],
                in_=x_grouped[(b, g)][:].rearrange("p t j -> p (t j)"),
            )

        def mean_and_std(b):
            halves = stats[b][:].rearrange("p r (h s) -> p (r h) s", s=3)
            half_mean = halves[:, :, 1]
            half_dev = halves[:, :, 2]
            mean_sq = two.tile([P, 2 * ROWS], F32, tag="mean_sq")
            nc.vector.tensor_tensor(out=mean_sq[:], in0=half_mean, in1=half_mean, op=ALU.mult)
            half_sq = two.tile([P, 2 * ROWS], F32, tag="half_sq")
            nc.vector.scalar_tensor_tensor(
                out=half_sq[:], in0=mean_sq[:], scalar=256.0, in1=half_dev,
                op0=ALU.mult, op1=ALU.add,
            )
            sum_sq = two.tile([P, ROWS], F32, tag="sum_sq")
            nc.vector.tensor_reduce(
                out=sum_sq[:], in_=half_sq[:].rearrange("p (r h) -> p r h", h=2),
                axis=AX.X, op=ALU.add,
            )
            sum_mean = two.tile([P, ROWS], F32, tag="sum_mean")
            nc.vector.tensor_reduce(
                out=sum_mean[:], in_=half_mean.rearrange("p (r h) -> p r h", h=2),
                axis=AX.X, op=ALU.add,
            )
            mean0 = two.tile([P, ROWS], F32, tag="mean0")
            nc.vector.tensor_scalar_mul(
                out=mean0[:], in0=sum_mean[:], scalar1=inv_sum_256[:, b : b + 1]
            )
            mean0_sq = two.tile([P, ROWS], F32, tag="mean0_sq")
            nc.vector.tensor_tensor(out=mean0_sq[:], in0=mean0[:], in1=mean0[:], op=ALU.mult)
            var0 = two.tile([P, ROWS], F32, tag="var0")
            nc.vector.scalar_tensor_tensor(
                out=var0[:], in0=sum_sq[:], scalar=inv_sum[:, b : b + 1], in1=mean0_sq[:],
                op0=ALU.mult, op1=ALU.subtract,
            )
            var0_floor = two.tile([P, ROWS], F32, tag="var0_floor")
            nc.vector.tensor_scalar_max(out=var0_floor[:], in0=var0[:], scalar1=EPS_STD)
            nc.gpsimd.tensor_tensor(
                out=stat_in[:, X_PASSES : 2 * X_PASSES, b, :],
                in0=var0_floor[:].rearrange("p (g j) -> p g j", j=SLOTS),
                in1=half[:].rearrange("p (g j) -> p g j", j=SLOTS),
                op=ALU.pow,
            )
            nc.vector.tensor_copy(
                out=stat_in[:, 0:X_PASSES, b, :],
                in_=mean0[:].rearrange("p (g j) -> p g j", j=SLOTS),
            )

        def stat_product(b):
            stat_codes = two.tile([P, 8 * STAT_STEP], U32, tag="stat_codes", align_bytes=64)
            stat_scales = two.tile([P, 8 * STAT_STEP], U8, tag="stat_scales", align_bytes=64)
            nc.vector.quantize_mx(
                out=stat_codes[:].bitcast(FP8X4),
                scales=stat_scales[:],
                in_=stat_in[:].rearrange("p s n j -> p (s n j)"),
            )
            product = ps_mx.tile([P, H_TILES, P], F32, tag="mx")
            stat_ps[b] = product
            for ht in range(H_TILES):
                for s in range(2 * X_PASSES):
                    nc.tensor.matmul_mx(
                        out=product[:, ht, :],
                        lhsT=w_codes[:, X_PASSES + s, P * ht : P * (ht + 1)].bitcast(FP8X4),
                        lhsT_scale=w_scales[:, X_PASSES + s, P * ht : P * (ht + 1)],
                        rhs=stat_codes[:, STAT_STEP * s : STAT_STEP * s + P].bitcast(FP8X4),
                        rhs_scale=stat_scales[:, STAT_STEP * s : STAT_STEP * s + P],
                        start=(s == 0),
                        stop=(s == 2 * X_PASSES - 1),
                    )

        def main_product(b):
            bias = two.tile([P, H_TILES], F32, tag="bias")
            nc.vector.tensor_tensor(
                out=bias[:], in0=stat_ps[b][:, :, b], in1=params[:, 0:4], op=ALU.add
            )
            x_codes, x_scales = x_quant[b]
            u = three.tile([P, H_TILES, T], F32, tag="u")
            relu_out[b] = u
            for ht in range(H_TILES):
                acc = ps_mx.tile([P, T], F32, tag="mx")
                for g in range(X_PASSES):
                    nc.tensor.matmul_mx(
                        out=acc[:],
                        lhsT=w_codes[:, g, P * ht : P * (ht + 1)].bitcast(FP8X4),
                        lhsT_scale=w_scales[:, g, P * ht : P * (ht + 1)],
                        rhs=x_codes[:, g, :].bitcast(FP8X4),
                        rhs_scale=x_scales[:, g, :],
                        start=(g == 0),
                        stop=(g == X_PASSES - 1),
                    )
                nc.scalar.activation(
                    out=u[:, ht, :], in_=acc[:], func=ACT.Relu, bias=bias[:, ht : ht + 1], scale=1.0
                )

        def layer_norm(b):
            u = relu_out[b]
            normed = two.tile([P, T_TILES, H], F32, tag="normed")
            for pair in range(2):
                ln_stats = four.tile([P, 2, 6], F32, tag="ln_stats")
                mean_var = four.tile([P, 2, 2], F32, tag="mean_var")
                banks = []
                for i in range(2):
                    tb = 2 * pair + i
                    u_t = ps_first.tile([P, H], F32, tag="first")
                    for ht in range(H_TILES):
                        nc.tensor.transpose(
                            u_t[:, P * ht : P * (ht + 1)], u[:, ht, P * tb : P * (tb + 1)],
                            ident_f32[:],
                        )
                    nc.vector.bn_stats(out=ln_stats[:, i, :], in_=u_t[:])
                    nc.vector.bn_aggr(out=mean_var[:, i, :], in_=ln_stats[:, i, :])
                    banks.append(u_t)
                var_eps = four.tile([P, 2], F32, tag="var_eps")
                nc.vector.tensor_scalar_add(out=var_eps[:], in0=mean_var[:, :, 1], scalar1=EPS_LN)
                neg_mean = four.tile([P, 2], F32, tag="neg_mean")
                nc.vector.tensor_scalar_mul(out=neg_mean[:], in0=mean_var[:, :, 0], scalar1=-1.0)
                rstd = four.tile([P, 2], F32, tag="rstd")
                nc.gpsimd.tensor_tensor(
                    out=rstd[:], in0=var_eps[:], in1=minus_half[:, 0:2], op=ALU.pow
                )
                shift = four.tile([P, 2], F32, tag="shift")
                nc.gpsimd.tensor_tensor(out=shift[:], in0=neg_mean[:], in1=rstd[:], op=ALU.mult)
                for i in range(2):
                    nc.scalar.activation(
                        out=normed[:, 2 * pair + i, :], in_=banks[i][:], func=ACT.Identity,
                        scale=rstd[:, i : i + 1], bias=shift[:, i : i + 1],
                    )
            for ht in range(H_TILES):
                back = ps_back.tile([P, T], F32, tag="back")
                for tb in range(T_TILES):
                    nc.tensor.transpose(
                        back[:, P * tb : P * (tb + 1)], normed[:, tb, P * ht : P * (ht + 1)],
                        ident_f32[:],
                    )
                result = four.tile([P, T], F32, tag="result")
                nc.scalar.activation(
                    out=result[:], in_=back[:], func=ACT.Tanh,
                    scale=params[:, 4 + ht : 5 + ht], bias=params[:, 8 + ht : 9 + ht],
                )
                nc.sync.dma_start(out=out[b, P * ht : P * (ht + 1), :], in_=result[:])

        for g in range(X_PASSES):
            group_x(0, g)
            masked_stats(0, g)
        x_tiles.append(load_x(2))
        nc.vector.reciprocal(out=inv_sum[:], in_=mask_sum[:])
        nc.vector.tensor_scalar_mul(out=inv_sum_256[:], in0=inv_sum[:], scalar1=256.0)
        mean_and_std(0)
        for g in range(W_PASSES):
            transpose_w(g)
            quantise_w(g)
            if g == X_PASSES - 1:
                x_tiles.append(load_x(3))
        for g in range(X_PASSES):
            quantise_x(0, g)
        param_ps = ps_mx.tile([P, P], BF16, tag="mx")
        nc.tensor.transpose(param_ps[:], param_rows[:], ident_bf16[:])
        nc.vector.tensor_copy(out=params[:], in_=param_ps[:, 0:12])
        stat_product(0)
        main_product(0)
        for b in range(1, B):
            for g in range(X_PASSES):
                group_x(b, g)
                masked_stats(b, g)
                if b == 3 and g == 0:
                    layer_norm(1)
            if b == 2:
                layer_norm(0)
            mean_and_std(b)
            for g in range(X_PASSES):
                quantise_x(b, g)
            stat_product(b)
            if b == 3:
                layer_norm(2)
            main_product(b)
        layer_norm(3)
